import numpy as np
import ml_dtypes


def mxq(x, axis, fmt="e4m3"):
    dtype, down = {"e4m3": (ml_dtypes.float8_e4m3fn, 7), "e5m2": (ml_dtypes.float8_e5m2, 14)}[fmt]
    v = np.moveaxis(np.asarray(x, np.float32).astype(ml_dtypes.bfloat16).astype(np.float64), axis, -1)
    blocks = v.reshape(v.shape[:-1] + (-1, 32))
    amax = np.abs(blocks).max(-1, keepdims=True)
    byte = np.maximum(np.where(amax > 0, np.frexp(amax)[1] - 1 + 127, 0) - down, 1)
    scale = np.exp2(byte - 127.0)
    codes = (blocks / scale).astype(np.float32).astype(dtype).astype(np.float64)
    return np.moveaxis((codes * scale).reshape(v.shape), -1, axis)


WIDE = False


def mx_kscale(k):
    if not WIDE:
        return np.ones(k)
    levels = np.array([10, -10, 5, -5, 0])
    a = np.random.permutation(np.resize(levels, k // 512 * 4)).reshape(k // 512, 4)
    idx = np.arange(k)
    return np.exp2(a[idx // 512, idx % 128 // 32])


BF16 = ml_dtypes.bfloat16


def bf(x):
    return np.asarray(x, np.float32).astype(BF16)


def f64(x):
    return np.asarray(x).astype(np.float64)


E2M1 = np.array([0.0, 0.5, 1.0, 1.5, 2.0, 3.0, 4.0, 6.0, -0.0, -0.5, -1.0, -1.5, -2.0, -3.0, -4.0, -6.0])


def pack_weight(w, fmt):
    k, n = w.shape
    w = f64(bf(w)).reshape(k // 32, 32, n)
    amax = np.abs(w).max(1)
    if fmt == "e4m3":
        byte = np.frexp(amax)[1] - 1 + 127 - 7
    else:
        mant, ex = np.frexp(amax / 6.0)
        byte = np.where(mant > 0.5, ex, ex - 1) + 127
    byte = np.clip(np.where(amax > 0, byte, 1), 1, 254)
    scaled = (w * np.exp2(127.0 - byte)[:, None, :]).reshape(k, n).astype(np.float32)
    by_word = np.ascontiguousarray(scaled.reshape(k // 512, 128, 4, n).transpose(0, 1, 3, 2))
    if fmt == "e4m3":
        words = by_word.astype(ml_dtypes.float8_e4m3fn).view(np.uint8)
    else:
        c = by_word.astype(ml_dtypes.float4_e2m1fn).view(np.uint8) & 0xF
        words = c[..., 0::2] | (c[..., 1::2] << 4)
    return np.ascontiguousarray(words), np.ascontiguousarray(byte.astype(np.uint8).reshape(k // 512, 16, n))


def unpack_weight(words, scales, fmt):
    g, p, n, _ = words.shape
    if fmt == "e4m3":
        vals = np.ascontiguousarray(words).view(ml_dtypes.float8_e4m3fn).astype(np.float64)
    else:
        nib = np.empty((g, p, n, 4), np.uint8)
        nib[..., 0::2] = words & 0xF
        nib[..., 1::2] = words >> 4
        vals = E2M1[nib]
    vals = vals * np.repeat(np.exp2(scales.astype(np.float64) - 127.0), 8, axis=1)[..., None]
    return vals.transpose(0, 1, 3, 2).reshape(g * 512, n)

def pack4(w):
    words, scales = pack_weight(w, "e2m1")
    return words.reshape(words.shape[0], 128, -1), scales


def unpack4(words, scales):
    return unpack_weight(words.reshape(words.shape[0], 128, -1, 2), scales, "e2m1")


B, D, F0, F1, F2, F3, P = 4096, 512, 512, 512, 256, 128, 200


def relu(v):
    return np.maximum(v, 0.0)


def neg_l1(feat, pr):
    return -np.stack([np.abs(feat - row).sum(-1) for row in pr], axis=1)


def setup_inputs():
    s = mx_kscale(F1)
    t = mx_kscale(F0)
    x = bf(np.random.standard_normal((B, D)))
    aW = np.random.standard_normal((D, D)) * 0.7 / np.sqrt(D)
    ab = bf(np.random.standard_normal(D) * 0.5)
    h_up = bf(np.maximum(np.random.standard_normal((B, F1)), 0.0) * 1.4 * s)
    h_skip = bf(np.maximum(np.random.standard_normal((B, F1)), 0.0) * 1.4 * s)
    Wu2 = np.random.standard_normal((F0, F1)) / np.sqrt(F1) / s[None, :] * t[:, None]
    bu2 = bf(np.random.standard_normal(F0) * 0.8 * t)
    Wu3 = np.random.standard_normal((D, F0)) * 1.4 / np.sqrt(F0) / t[None, :]
    bu3 = bf(np.random.standard_normal(D) * 0.8)
    protos = bf(np.random.standard_normal((P, D)))
    aW_words, aW_scales = pack4(np.ascontiguousarray(aW.T))
    Wu2_words, Wu2_scales = pack4(np.ascontiguousarray(Wu2.T))
    Wu3_words, Wu3_scales = pack4(np.ascontiguousarray(Wu3.T))
    return {
        "x": x,
        "aW_words": aW_words,
        "aW_scales": aW_scales,
        "ab": ab,
        "h_up": h_up,
        "h_skip": h_skip,
        "Wu2_words": Wu2_words,
        "Wu2_scales": Wu2_scales,
        "bu2": bu2,
        "Wu3_words": Wu3_words,
        "Wu3_scales": Wu3_scales,
        "bu3": bu3,
        "protos": protos,
    }


def reference(x, aW_words, aW_scales, ab, h_up, h_skip, Wu2_words, Wu2_scales, bu2, Wu3_words, Wu3_scales, bu3, protos):
    xf = f64(x)
    z = f64(h_up) + f64(h_skip)
    u2 = relu((mxq(z, 1, "e4m3") @ unpack4(Wu2_words, Wu2_scales)) + f64(bu2))
    u3 = relu((mxq(u2, 1, "e4m3") @ unpack4(Wu3_words, Wu3_scales)) + f64(bu3))
    feat = xf + ((mxq(xf, 1, "e4m3") @ unpack4(aW_words, aW_scales)) + f64(ab)) + u3
    return neg_l1(feat, f64(protos))

@@ -1,0 +1,342 @@
+from contextlib import ExitStack
+
+import concourse.mybir as mybir
+from concourse.masks import make_identity
+
+F32 = mybir.dt.float32
+BF16 = mybir.dt.bfloat16
+I32 = mybir.dt.int32
+U32 = mybir.dt.uint32
+U8 = mybir.dt.uint8
+FP8X4 = mybir.dt.float8_e4m3fn_x4
+FP4X4 = mybir.dt.float4_e2m1fn_x4
+ADD = mybir.AluOpType.add
+MAX = mybir.AluOpType.max
+MULT = mybir.AluOpType.mult
+ABS = mybir.ActivationFunctionType.Abs
+RELU = mybir.ActivationFunctionType.Relu
+IDENTITY = mybir.ActivationFunctionType.Identity
+
+P = 128
+PACK = 4
+BATCH = 4096
+D = 512
+CHUNKS = D // P
+PROTOS = 200
+TILES = BATCH // P
+GROUP = 4
+GROUP_COLS = GROUP * P
+LOAD_TILES = 8
+BLOCK_TILES = 8
+BLOCK_COLS = BLOCK_TILES * P
+BANK = 512
+A_W, W_U2, W_U3 = 0, 1, 2
+
+FLOPS = 3 * 2 * BATCH * D * D + 3 * BATCH * PROTOS * D
+
+
+def flip_bf16(nc, psum, ident, source, grouped, relu):
+    for pair in range(GROUP // 2):
+        flipped = psum.tile([P, PACK, 2 * P], BF16, tag="flip")
+        for j in range(2):
+            for t in range(PACK):
+                nc.tensor.transpose(flipped[:, t, P * j : P * (j + 1)], source(2 * pair + j, t), ident[:])
+        dst = grouped[:, 2 * P * pair : 2 * P * (pair + 1), :]
+        src = flipped[:].rearrange("q t b -> q b t")
+        if relu:
+            nc.scalar.activation(out=dst, in_=src, func=RELU)
+        else:
+            nc.scalar.copy(out=dst, in_=src)
+
+
+def quantise(nc, pool, grouped, name):
+    codes = pool.tile([P, GROUP_COLS], U32, tag="codes_" + name, align_bytes=64)
+    scales = pool.tile([P, GROUP_COLS], U8, tag="scales_" + name, align_bytes=64)
+    nc.vector.quantize_mx(
+        out=codes[:].bitcast(FP8X4),
+        scales=scales[:],
+        in_=grouped[:].rearrange("q b t -> q (b t)"),
+    )
+    return codes, scales
+
+
+def tile_prototypelearnerv4_pa_t_kernel(
+    tc, x, aW_words, aW_scales, ab, h_up, h_skip, Wu2_words, Wu2_scales, bu2, Wu3_words, Wu3_scales, bu3, protos, out
+):
+    nc = tc.nc
+    by_tile = "(r i) d -> r i d"
+    x_rows = x.rearrange(by_tile, i=TILES)
+    h_up_rows = h_up.rearrange(by_tile, i=TILES)
+    h_skip_rows = h_skip.rearrange(by_tile, i=TILES)
+    out_rows = out.rearrange(by_tile, i=TILES)
+
+    with ExitStack() as whole:
+        keep = whole.enter_context(tc.tile_pool(name="keep", bufs=1))
+        feat = keep.tile([P, CHUNKS, BATCH], F32)
+        words = keep.tile([P, 3, 2 * D], U8, align_bytes=64)
+        planes = keep.tile([P, 3, D], U8, align_bytes=64)
+        ident_bf = keep.tile([P, P], BF16)
+        ident_f = keep.tile([P, P], F32)
+        ones = keep.tile([P, P], F32)
+        bu2_all = keep.tile([P, D], BF16)
+        bias_rows = keep.tile([P, P], BF16)
+        bias_cols = keep.tile([P, 2 * CHUNKS], F32)
+        proto_rows = keep.tile([P, 2, D], BF16)
+        proto_t = keep.tile([P, CHUNKS, PROTOS], F32)
+        proto_neg_half = keep.tile([P, 2, PROTOS], F32)
+        proto_sums = keep.tile([P, PROTOS], F32)
+        feat_sums = keep.tile([P, TILES], F32)
+
+        nc.vector.memset(planes[:].rearrange("q w n -> q (w n)").bitcast(I32), 0)
+        nc.vector.memset(bias_rows[:], 0.0)
+        nc.vector.memset(proto_rows[:], 0.0)
+        nc.vector.memset(ones[:], 1.0)
+        make_identity(nc, ident_bf[:])
+        make_identity(nc, ident_f[:])
+
+        with ExitStack() as front:
+            loads = front.enter_context(tc.tile_pool(name="loads", bufs=2))
+            work = front.enter_context(tc.tile_pool(name="work", bufs=2))
+            flips = front.enter_context(tc.psum_pool(name="flips", bufs=3))
+            products = front.enter_context(tc.psum_pool(name="products", bufs=4))
+            columns = front.enter_context(tc.psum_pool(name="columns", bufs=1))
+            feat_sums_ps = columns.tile([P, 2, TILES], F32)
+
+            def fetch(load):
+                rows = slice(LOAD_TILES * load, LOAD_TILES * (load + 1))
+                hu = loads.tile([P, LOAD_TILES, D], BF16, tag="hu")
+                hs = loads.tile([P, LOAD_TILES, D], BF16, tag="hs")
+                xs = loads.tile([P, LOAD_TILES, D], BF16, tag="xs")
+                nc.sync.dma_start(out=hu[:], in_=h_up_rows[:, rows, :])
+                nc.sync.dma_start(out=hs[:], in_=h_skip_rows[:, rows, :])
+                nc.sync.dma_start(out=xs[:], in_=x_rows[:, rows, :])
+                return hu, hs, xs
+
+            fetched = fetch(0)
+
+            given = ((A_W, aW_words, aW_scales), (W_U2, Wu2_words, Wu2_scales), (W_U3, Wu3_words, Wu3_scales))
+            for w, w_words, w_scales in given:
+                nc.sync.dma_start(out=words[:, w, :].bitcast(I32), in_=w_words[0].bitcast(I32))
+            for w, w_words, w_scales in given:
+                for quad in range(4):
+                    nc.sync.dma_start(
+                        out=planes[32 * quad : 32 * quad + 4, w, :].bitcast(I32),
+                        in_=w_scales[0, 4 * quad : 4 * quad + 4, :].bitcast(I32),
+                    )
+            nc.scalar.dma_start(out=bu2_all[:], in_=bu2.partition_broadcast(P))
+            nc.scalar.dma_start(out=bias_rows[0:CHUNKS, :], in_=bu3.rearrange("(c q) -> c q", q=P))
+            nc.scalar.dma_start(out=bias_rows[CHUNKS : 2 * CHUNKS, :], in_=ab.rearrange("(c q) -> c q", q=P))
+            nc.scalar.dma_start(out=proto_rows[:, 0, :], in_=protos[0:P, :])
+            nc.scalar.dma_start(out=proto_rows[0 : PROTOS - P, 1, :], in_=protos[P:PROTOS, :])
+
+            bias_t = flips.tile([P, P], BF16, tag="flip")
+            nc.tensor.transpose(bias_t[:], bias_rows[:], ident_bf[:])
+            nc.vector.tensor_copy(out=bias_cols[:], in_=bias_t[:, 0 : 2 * CHUNKS])
+            proto_ps = flips.tile([P, CHUNKS, 2 * P], BF16, tag="flip")
+            for c in range(CHUNKS):
+                for half in range(2):
+                    nc.tensor.transpose(
+                        proto_ps[:, c, P * half : P * (half + 1)],
+                        proto_rows[:, half, P * c : P * (c + 1)],
+                        ident_bf[:],
+                    )
+            nc.vector.tensor_copy(out=proto_t[:], in_=proto_ps[:, :, 0:PROTOS])
+            nc.vector.tensor_scalar(
+                out=proto_neg_half[:], in0=proto_ps[:, 0:2, 0:PROTOS], scalar1=-0.5, scalar2=None, op0=MULT
+            )
+            proto_sums_ps = flips.tile([P, PROTOS], F32, tag="flip")
+            nc.tensor.matmul(out=proto_sums_ps[:], lhsT=ones[:], rhs=proto_t[:, 2, :], start=True, stop=False)
+            nc.tensor.matmul(out=proto_sums_ps[:], lhsT=ones[:], rhs=proto_t[:, 3, :], start=False, stop=True)
+            nc.vector.tensor_copy(out=proto_sums[:], in_=proto_sums_ps[:])
+
+            for load in range(TILES // LOAD_TILES):
+                hu, hs, xs = fetched
+                if load + 1 < TILES // LOAD_TILES:
+                    fetched = fetch(load + 1)
+
+                for part in range(LOAD_TILES // GROUP):
+                    first = GROUP * part
+                    group = (LOAD_TILES // GROUP) * load + part
+                    cols = slice(GROUP_COLS * group, GROUP_COLS * (group + 1))
+
+                    z = work.tile([P, GROUP, D], BF16, tag="z")
+                    nc.vector.tensor_tensor(
+                        out=z[:], in0=hu[:, first : first + GROUP, :], in1=hs[:, first : first + GROUP, :], op=ADD
+                    )
+                    z_grouped = work.tile([P, GROUP_COLS, PACK], BF16, tag="z_grouped", align_bytes=64)
+                    flip_bf16(nc, flips, ident_bf, lambda j, t: z[:, j, t:D:PACK], z_grouped, relu=False)
+                    z_codes, z_scales = quantise(nc, work, z_grouped, "z")
+
+                    x_grouped = work.tile([P, GROUP_COLS, PACK], BF16, tag="x_grouped", align_bytes=64)
+                    x_pairs = x_grouped[:].rearrange("q b t -> q (b t)").bitcast(F32).rearrange("q (b u) -> q b u", u=2)
+                    for pair in range(GROUP // 2):
+                        flipped = flips.tile([P, 2, 2 * P], F32, tag="flip")
+                        for j in range(2):
+                            x_words = xs[:, first + 2 * pair + j, :].bitcast(F32)
+                            for u in range(2):
+                                nc.tensor.transpose(flipped[:, u, P * j : P * (j + 1)], x_words[:, u : D // 2 : 2], ident_f[:])
+                        nc.scalar.copy(
+                            out=x_pairs[:, 2 * P * pair : 2 * P * (pair + 1), :],
+                            in_=flipped[:].rearrange("q u b -> q b u"),
+                        )
+                    x_codes, x_scales = quantise(nc, work, x_grouped, "x")
+
+                    pre_u2 = work.tile([P, GROUP, PACK, P], BF16, tag="pre_u2")
+                    for j in range(GROUP):
+                        product = products.tile([P, D], F32, tag="product")
+                        nc.tensor.matmul_mx(
+                            out=product[:],
+                            lhsT=z_codes[:, P * j : P * (j + 1)].bitcast(FP8X4),
+                            lhsT_scale=z_scales[:, P * j : P * (j + 1)],
+                            rhs=words[:, W_U2, :].bitcast(FP4X4),
+                            rhs_scale=planes[:, W_U2, :],
+                            start=True,
+                            stop=True,
+                        )
+                        nc.vector.tensor_tensor(
+                            out=pre_u2[:, j, :, :],
+                            in0=product[:].rearrange("b (q t) -> b t q", t=PACK),
+                            in1=bu2_all[:].rearrange("b (q t) -> b t q", t=PACK),
+                            op=ADD,
+                        )
+                    u2_grouped = work.tile([P, GROUP_COLS, PACK], BF16, tag="u2_grouped", align_bytes=64)
+                    flip_bf16(nc, flips, ident_bf, lambda j, t: pre_u2[:, j, t, :], u2_grouped, relu=True)
+                    u2_codes, u2_scales = quantise(nc, work, u2_grouped, "u2")
+
+                    for pair in range(CHUNKS // 2):
+                        x_t = flips.tile([P, 2, GROUP_COLS], BF16, tag="flip")
+                        for k in range(2):
+                            c = 2 * pair + k
+                            for j in range(GROUP):
+                                nc.tensor.transpose(
+                                    x_t[:, k, P * j : P * (j + 1)], xs[:, first + j, P * c : P * (c + 1)], ident_bf[:]
+                                )
+                        for k in range(2):
+                            c = 2 * pair + k
+                            up = products.tile([P, GROUP_COLS], F32, tag="product")
+                            nc.tensor.matmul_mx(
+                                out=up[:],
+                                lhsT=words[:, W_U3, 2 * P * c : 2 * P * (c + 1)].bitcast(FP4X4),
+                                lhsT_scale=planes[:, W_U3, P * c : P * (c + 1)],
+                                rhs=u2_codes[:].bitcast(FP8X4),
+                                rhs_scale=u2_scales[:],
+                                start=True,
+                                stop=True,
+                            )
+                            adapter = products.tile([P, GROUP_COLS], F32, tag="product")
+                            nc.tensor.matmul_mx(
+                                out=adapter[:],
+                                lhsT=words[:, A_W, 2 * P * c : 2 * P * (c + 1)].bitcast(FP4X4),
+                                lhsT_scale=planes[:, A_W, P * c : P * (c + 1)],
+                                rhs=x_codes[:].bitcast(FP8X4),
+                                rhs_scale=x_scales[:],
+                                start=True,
+                                stop=True,
+                            )
+                            u3 = work.tile([P, GROUP_COLS], F32, tag="u3")
+                            nc.scalar.activation(out=u3[:], in_=up[:], func=RELU, bias=bias_cols[:, c : c + 1])
+                            two = work.tile([P, GROUP_COLS], F32, tag="two")
+                            nc.vector.scalar_tensor_tensor(
+                                out=two[:],
+                                in0=adapter[:],
+                                scalar=bias_cols[:, CHUNKS + c : CHUNKS + c + 1],
+                                in1=u3[:],
+                                op0=ADD,
+                                op1=ADD,
+                            )
+                            nc.vector.tensor_tensor(out=feat[:, c, cols], in0=x_t[:, k, :], in1=two[:], op=ADD)
+
+                    for j in range(GROUP):
+                        i = GROUP * group + j
+                        for c in (2, 3):
+                            nc.tensor.matmul(
+                                out=feat_sums_ps[:, c - 2, i : i + 1],
+                                lhsT=feat[:, c, P * i : P * (i + 1)],
+                                rhs=ones[:, 0:1],
+                                start=True,
+                                stop=True,
+                            )
+            nc.vector.tensor_reduce(
+                out=feat_sums[:], in_=feat_sums_ps[:].rearrange("b c i -> b i c"), axis=mybir.AxisListType.X, op=ADD
+            )
+
+        with ExitStack() as distances:
+            halves = distances.enter_context(tc.tile_pool(name="halves", bufs=3))
+            runs = distances.enter_context(tc.tile_pool(name="runs", bufs=4))
+            results = distances.enter_context(tc.tile_pool(name="results", bufs=2))
+            banks = distances.enter_context(tc.psum_pool(name="banks", bufs=1))
+
+            for block in range(TILES // BLOCK_TILES):
+                start_col = BLOCK_COLS * block
+                feat_ps = {}
+                for c in (2, 3):
+                    for h in range(BLOCK_COLS // BANK):
+                        bank = banks.tile([P, BANK], F32, tag="feat_ps_%d_%d" % (c, h))
+                        nc.tensor.matmul(
+                            out=bank[:],
+                            lhsT=ident_f[:],
+                            rhs=feat[:, c, start_col + BANK * h : start_col + BANK * (h + 1)],
+                            start=True,
+                            stop=True,
+                        )
+                        feat_ps[(c, h)] = bank
+                sums = []
+                for s in range(BLOCK_TILES // 2):
+                    sums_bank = banks.tile([P, 2, PROTOS], F32, tag="sums_%d" % s)
+                    sums.append(sums_bank)
+
+                for p in range(PROTOS):
+                    half0 = halves.tile([P, BLOCK_COLS], F32, tag="half0")
+                    half1 = halves.tile([P, BLOCK_COLS], F32, tag="half1")
+                    both = halves.tile([P, BLOCK_COLS], F32, tag="both")
+                    block_cols = slice(start_col, start_col + BLOCK_COLS)
+                    nc.scalar.activation(
+                        out=half0[:], in_=feat[:, 0, block_cols], func=ABS, bias=proto_neg_half[:, 0, p : p + 1], scale=0.5
+                    )
+                    nc.scalar.activation(
+                        out=half1[:], in_=feat[:, 1, block_cols], func=ABS, bias=proto_neg_half[:, 1, p : p + 1], scale=0.5
+                    )
+                    nc.gpsimd.tensor_tensor(out=both[:], in0=half0[:], in1=half1[:], op=ADD)
+                    run2 = []
+                    for h in range(BLOCK_COLS // BANK):
+                        run = runs.tile([P, BANK], F32, tag="run2")
+                        nc.vector.scalar_tensor_tensor(
+                            out=run[:],
+                            in0=feat_ps[(2, h)][:],
+                            scalar=proto_t[:, 2, p : p + 1],
+                            in1=both[:, BANK * h : BANK * (h + 1)],
+                            op0=MAX,
+                            op1=ADD,
+                        )
+                        run2.append(run)
+                    for h in range(BLOCK_COLS // BANK):
+                        run = runs.tile([P, BANK], F32, tag="run3")
+                        nc.vector.scalar_tensor_tensor(
+                            out=run[:],
+                            in0=feat_ps[(3, h)][:],
+                            scalar=proto_t[:, 3, p : p + 1],
+                            in1=run2[h][:],
+                            op0=MAX,
+                            op1=ADD,
+                        )
+                        for q in range(BANK // P):
+                            j = (BANK // P) * h + q
+                            nc.tensor.matmul(
+                                out=sums[j // 2][:, j % 2, p : p + 1],
+                                lhsT=run[:, P * q : P * (q + 1)],
+                                rhs=ones[:, 0:1],
+                                start=True,
+                                stop=True,
+                            )
+
+                result = results.tile([P, BLOCK_TILES, PROTOS], F32, tag="result")
+                for j in range(BLOCK_TILES):
+                    i = BLOCK_TILES * block + j
+                    partial = results.tile([P, PROTOS], F32, tag="partial")
+                    nc.scalar.activation(
+                        out=partial[:], in_=sums[j // 2][:, j % 2, :], func=IDENTITY, bias=feat_sums[:, i : i + 1], scale=-2.0
+                    )
+                    nc.vector.tensor_tensor(out=result[:, j, :], in0=partial[:], in1=proto_sums[:], op=ADD)
+                nc.sync.dma_start(
+                    out=out_rows[:, BLOCK_TILES * block : BLOCK_TILES * (block + 1), :], in_=result[:]
+                )

@@ -13,7 +13,6 @@ FP4X4 = mybir.dt.float4_e2m1fn_x4
 ADD = mybir.AluOpType.add
 MAX = mybir.AluOpType.max
 MULT = mybir.AluOpType.mult
-ABS = mybir.ActivationFunctionType.Abs
 RELU = mybir.ActivationFunctionType.Relu
 IDENTITY = mybir.ActivationFunctionType.Identity
 
@@ -29,7 +28,9 @@ GROUP_COLS = GROUP * P
 LOAD_TILES = 8
 BLOCK_TILES = 8
 BLOCK_COLS = BLOCK_TILES * P
-BANK = 512
+ROUND = 2
+BANK_TILES = 4
+LAG = 4
 A_W, W_U2, W_U3 = 0, 1, 2
 
 FLOPS = 3 * 2 * BATCH * D * D + 3 * BATCH * PROTOS * D
@@ -82,8 +83,7 @@ def tile_prototypelearnerv4_pa_t_kernel(
         bias_rows = keep.tile([P, P], BF16)
         bias_cols = keep.tile([P, 2 * CHUNKS], F32)
         proto_rows = keep.tile([P, 2, D], BF16)
-        proto_t = keep.tile([P, CHUNKS, PROTOS], F32)
-        proto_neg_half = keep.tile([P, 2, PROTOS], F32)
+        proto_signed = keep.tile([P, CHUNKS, PROTOS], F32)
         proto_sums = keep.tile([P, PROTOS], F32)
         feat_sums = keep.tile([P, TILES], F32)
 
@@ -100,7 +100,7 @@ def tile_prototypelearnerv4_pa_t_kernel(
             flips = front.enter_context(tc.psum_pool(name="flips", bufs=3))
             products = front.enter_context(tc.psum_pool(name="products", bufs=4))
             columns = front.enter_context(tc.psum_pool(name="columns", bufs=1))
-            feat_sums_ps = columns.tile([P, 2, TILES], F32)
+            feat_sums_ps = columns.tile([P, CHUNKS, TILES], F32)
 
             def fetch(load):
                 rows = slice(LOAD_TILES * load, LOAD_TILES * (load + 1))
@@ -140,13 +140,19 @@ def tile_prototypelearnerv4_pa_t_kernel(
                         proto_rows[:, half, P * c : P * (c + 1)],
                         ident_bf[:],
                     )
-            nc.vector.tensor_copy(out=proto_t[:], in_=proto_ps[:, :, 0:PROTOS])
+            nc.vector.tensor_copy(out=proto_signed[:], in_=proto_ps[:, :, 0:PROTOS])
+            for c in (0, 2):
+                nc.vector.tensor_scalar(
+                    out=proto_signed[:, c, :], in0=proto_ps[:, c, 0:PROTOS], scalar1=-1.0, scalar2=None, op0=MULT
+                )
             nc.vector.tensor_scalar(
-                out=proto_neg_half[:], in0=proto_ps[:, 0:2, 0:PROTOS], scalar1=-0.5, scalar2=None, op0=MULT
+                out=proto_signed[:, 1, 0:PROTOS:2], in0=proto_ps[:, 1, 0:PROTOS:2], scalar1=-1.0, scalar2=None, op0=MULT
             )
             proto_sums_ps = flips.tile([P, PROTOS], F32, tag="flip")
-            nc.tensor.matmul(out=proto_sums_ps[:], lhsT=ones[:], rhs=proto_t[:, 2, :], start=True, stop=False)
-            nc.tensor.matmul(out=proto_sums_ps[:], lhsT=ones[:], rhs=proto_t[:, 3, :], start=False, stop=True)
+            for c in range(CHUNKS):
+                nc.tensor.matmul(
+                    out=proto_sums_ps[:], lhsT=ones[:], rhs=proto_signed[:, c, :], start=(c == 0), stop=(c == CHUNKS - 1)
+                )
             nc.vector.tensor_copy(out=proto_sums[:], in_=proto_sums_ps[:])
 
             for load in range(TILES // LOAD_TILES):
@@ -248,9 +254,9 @@ def tile_prototypelearnerv4_pa_t_kernel(
 
                     for j in range(GROUP):
                         i = GROUP * group + j
-                        for c in (2, 3):
+                        for c in range(CHUNKS):
                             nc.tensor.matmul(
-                                out=feat_sums_ps[:, c - 2, i : i + 1],
+                                out=feat_sums_ps[:, c, i : i + 1],
                                 lhsT=feat[:, c, P * i : P * (i + 1)],
                                 rhs=ones[:, 0:1],
                                 start=True,
@@ -261,82 +267,95 @@ def tile_prototypelearnerv4_pa_t_kernel(
             )
 
         with ExitStack() as distances:
-            halves = distances.enter_context(tc.tile_pool(name="halves", bufs=3))
-            runs = distances.enter_context(tc.tile_pool(name="runs", bufs=4))
+            starts = distances.enter_context(tc.tile_pool(name="starts", bufs=10))
+            runs = distances.enter_context(tc.tile_pool(name="runs", bufs=6))
             results = distances.enter_context(tc.tile_pool(name="results", bufs=2))
-            banks = distances.enter_context(tc.psum_pool(name="banks", bufs=1))
+            banks = distances.enter_context(tc.psum_pool(name="banks", bufs=2 * ROUND))
+            distances.enter_context(tc.manual_schedule())
 
-            for block in range(TILES // BLOCK_TILES):
-                start_col = BLOCK_COLS * block
-                feat_ps = {}
-                for c in (2, 3):
-                    for h in range(BLOCK_COLS // BANK):
-                        bank = banks.tile([P, BANK], F32, tag="feat_ps_%d_%d" % (c, h))
-                        nc.tensor.matmul(
-                            out=bank[:],
-                            lhsT=ident_f[:],
-                            rhs=feat[:, c, start_col + BANK * h : start_col + BANK * (h + 1)],
-                            start=True,
-                            stop=True,
-                        )
-                        feat_ps[(c, h)] = bank
-                sums = []
-                for s in range(BLOCK_TILES // 2):
-                    sums_bank = banks.tile([P, 2, PROTOS], F32, tag="sums_%d" % s)
-                    sums.append(sums_bank)
+            def chains_of(p):
+                if p % 2 == 0:
+                    return ((0,), (1,), (2, 3))
+                return ((0, 1), (2, 3))
 
-                for p in range(PROTOS):
-                    half0 = halves.tile([P, BLOCK_COLS], F32, tag="half0")
-                    half1 = halves.tile([P, BLOCK_COLS], F32, tag="half1")
-                    both = halves.tile([P, BLOCK_COLS], F32, tag="both")
-                    block_cols = slice(start_col, start_col + BLOCK_COLS)
-                    nc.scalar.activation(
-                        out=half0[:], in_=feat[:, 0, block_cols], func=ABS, bias=proto_neg_half[:, 0, p : p + 1], scale=0.5
-                    )
-                    nc.scalar.activation(
-                        out=half1[:], in_=feat[:, 1, block_cols], func=ABS, bias=proto_neg_half[:, 1, p : p + 1], scale=0.5
-                    )
-                    nc.gpsimd.tensor_tensor(out=both[:], in0=half0[:], in1=half1[:], op=ADD)
-                    run2 = []
-                    for h in range(BLOCK_COLS // BANK):
-                        run = runs.tile([P, BANK], F32, tag="run2")
-                        nc.vector.scalar_tensor_tensor(
-                            out=run[:],
-                            in0=feat_ps[(2, h)][:],
-                            scalar=proto_t[:, 2, p : p + 1],
-                            in1=both[:, BANK * h : BANK * (h + 1)],
-                            op0=MAX,
-                            op1=ADD,
+            def add_lanes(sums, waiting):
+                for p, lanes in waiting:
+                    for h in range(BLOCK_TILES // BANK_TILES):
+                        nc.vector.tensor_reduce(
+                            out=sums[:, BANK_TILES * h : BANK_TILES * (h + 1), p],
+                            in_=lanes[h][:],
+                            axis=mybir.AxisListType.X,
+                            op=ADD,
                         )
-                        run2.append(run)
-                    for h in range(BLOCK_COLS // BANK):
-                        run = runs.tile([P, BANK], F32, tag="run3")
-                        nc.vector.scalar_tensor_tensor(
-                            out=run[:],
-                            in0=feat_ps[(3, h)][:],
-                            scalar=proto_t[:, 3, p : p + 1],
-                            in1=run2[h][:],
-                            op0=MAX,
-                            op1=ADD,
-                        )
-                        for q in range(BANK // P):
-                            j = (BANK // P) * h + q
-                            nc.tensor.matmul(
-                                out=sums[j // 2][:, j % 2, p : p + 1],
-                                lhsT=run[:, P * q : P * (q + 1)],
-                                rhs=ones[:, 0:1],
-                                start=True,
-                                stop=True,
-                            )
 
+            def finish(block, sums):
                 result = results.tile([P, BLOCK_TILES, PROTOS], F32, tag="result")
                 for j in range(BLOCK_TILES):
                     i = BLOCK_TILES * block + j
-                    partial = results.tile([P, PROTOS], F32, tag="partial")
                     nc.scalar.activation(
-                        out=partial[:], in_=sums[j // 2][:, j % 2, :], func=IDENTITY, bias=feat_sums[:, i : i + 1], scale=-2.0
+                        out=sums[:, j, :], in_=sums[:, j, :], func=IDENTITY, bias=feat_sums[:, i : i + 1], scale=-2.0
                     )
-                    nc.vector.tensor_tensor(out=result[:, j, :], in0=partial[:], in1=proto_sums[:], op=ADD)
-                nc.sync.dma_start(
-                    out=out_rows[:, BLOCK_TILES * block : BLOCK_TILES * (block + 1), :], in_=result[:]
+                nc.vector.tensor_tensor(
+                    out=result[:],
+                    in0=sums[:],
+                    in1=proto_sums[:].unsqueeze(1).to_broadcast([P, BLOCK_TILES, PROTOS]),
+                    op=ADD,
                 )
+                nc.sync.dma_start(out=out_rows[:, BLOCK_TILES * block : BLOCK_TILES * (block + 1), :], in_=result[:])
+
+            previous = None
+            for block in range(TILES // BLOCK_TILES):
+                block_cols = slice(BLOCK_COLS * block, BLOCK_COLS * (block + 1))
+                sums = results.tile([P, BLOCK_TILES, PROTOS], F32, tag="sums")
+                waiting = []
+                for first_p in range(0, PROTOS, ROUND):
+                    round_protos = range(first_p, first_p + ROUND)
+                    live = {}
+                    for p in round_protos:
+                        for chain in chains_of(p):
+                            c = chain[0]
+                            run = starts.tile([P, BLOCK_COLS], F32, tag="start")
+                            nc.scalar.activation(
+                                out=run[:], in_=feat[:, c, block_cols], func=RELU, bias=proto_signed[:, c, p : p + 1]
+                            )
+                            live[(p, chain)] = run
+                    for p in round_protos:
+                        for chain in chains_of(p):
+                            for c in chain[1:]:
+                                run = runs.tile([P, BLOCK_COLS], F32, tag="run")
+                                nc.vector.scalar_tensor_tensor(
+                                    out=run[:],
+                                    in0=feat[:, c, block_cols],
+                                    scalar=proto_signed[:, c, p : p + 1],
+                                    in1=live[(p, chain)][:],
+                                    op0=MAX,
+                                    op1=ADD,
+                                )
+                                live[(p, chain)] = run
+                    filled = []
+                    for p in round_protos:
+                        chains = chains_of(p)
+                        lanes = []
+                        for h in range(BLOCK_TILES // BANK_TILES):
+                            bank = banks.tile([P, BANK_TILES, P], F32, tag="lanes_%d" % h)
+                            for q in range(BANK_TILES):
+                                j = BANK_TILES * h + q
+                                for chain in chains:
+                                    nc.tensor.matmul(
+                                        out=bank[:, q, :],
+                                        lhsT=live[(p, chain)][:, P * j : P * (j + 1)],
+                                        rhs=ident_f[:],
+                                        start=(chain == chains[0]),
+                                        stop=(chain == chains[-1]),
+                                        is_transpose=True,
+                                    )
+                            lanes.append(bank)
+                        filled.append((p, lanes))
+                    add_lanes(sums, waiting)
+                    waiting = filled
+                    if previous is not None and first_p >= LAG:
+                        finish(*previous)
+                        previous = None
+                add_lanes(sums, waiting)
+                previous = (block, sums)
+            finish(*previous)

@@ -29,6 +29,7 @@ LOAD_TILES = 8
 BLOCK_TILES = 8
 BLOCK_COLS = BLOCK_TILES * P
 ROUND = 2
+SCALAR_CHUNKS = 2
 BANK_TILES = 4
 LAG = 4
 A_W, W_U2, W_U3 = 0, 1, 2
@@ -141,12 +142,12 @@ def tile_prototypelearnerv4_pa_t_kernel(
                         ident_bf[:],
                     )
             nc.vector.tensor_copy(out=proto_signed[:], in_=proto_ps[:, :, 0:PROTOS])
-            for c in (0, 2):
-                nc.vector.tensor_scalar(
-                    out=proto_signed[:, c, :], in0=proto_ps[:, c, 0:PROTOS], scalar1=-1.0, scalar2=None, op0=MULT
-                )
             nc.vector.tensor_scalar(
-                out=proto_signed[:, 1, 0:PROTOS:2], in0=proto_ps[:, 1, 0:PROTOS:2], scalar1=-1.0, scalar2=None, op0=MULT
+                out=proto_signed[:, 0:SCALAR_CHUNKS, :],
+                in0=proto_ps[:, 0:SCALAR_CHUNKS, 0:PROTOS],
+                scalar1=-1.0,
+                scalar2=None,
+                op0=MULT,
             )
             proto_sums_ps = flips.tile([P, PROTOS], F32, tag="flip")
             for c in range(CHUNKS):
@@ -268,15 +269,13 @@ def tile_prototypelearnerv4_pa_t_kernel(
 
         with ExitStack() as distances:
             starts = distances.enter_context(tc.tile_pool(name="starts", bufs=10))
-            runs = distances.enter_context(tc.tile_pool(name="runs", bufs=6))
+            runs = distances.enter_context(tc.tile_pool(name="runs", bufs=10))
             results = distances.enter_context(tc.tile_pool(name="results", bufs=2))
             banks = distances.enter_context(tc.psum_pool(name="banks", bufs=2 * ROUND))
             distances.enter_context(tc.manual_schedule())
 
             def chains_of(p):
-                if p % 2 == 0:
-                    return ((0,), (1,), (2, 3))
-                return ((0, 1), (2, 3))
+                return ((0,), (1,), (2,), (3,))
 
             def add_lanes(sums, waiting):
                 for p, lanes in waiting:
@@ -314,10 +313,20 @@ def tile_prototypelearnerv4_pa_t_kernel(
                     for p in round_protos:
                         for chain in chains_of(p):
                             c = chain[0]
-                            run = starts.tile([P, BLOCK_COLS], F32, tag="start")
-                            nc.scalar.activation(
-                                out=run[:], in_=feat[:, c, block_cols], func=RELU, bias=proto_signed[:, c, p : p + 1]
-                            )
+                            if c < SCALAR_CHUNKS:
+                                run = starts.tile([P, BLOCK_COLS], F32, tag="start")
+                                nc.scalar.activation(
+                                    out=run[:], in_=feat[:, c, block_cols], func=RELU, bias=proto_signed[:, c, p : p + 1]
+                                )
+                            else:
+                                run = runs.tile([P, BLOCK_COLS], F32, tag="run")
+                                nc.vector.tensor_scalar(
+                                    out=run[:],
+                                    in0=feat[:, c, block_cols],
+                                    scalar1=proto_signed[:, c, p : p + 1],
+                                    scalar2=None,
+                                    op0=MAX,
+                                )
                             live[(p, chain)] = run
                     for p in round_protos:
                         for chain in chains_of(p):

@@ -30,6 +30,7 @@ BLOCK_TILES = 8
 BLOCK_COLS = BLOCK_TILES * P
 ROUND = 2
 SCALAR_CHUNKS = 2
+LONG_EVERY = 4
 BANK_TILES = 4
 LAG = 4
 A_W, W_U2, W_U3 = 0, 1, 2
@@ -86,7 +87,6 @@ def tile_prototypelearnerv4_pa_t_kernel(
         proto_rows = keep.tile([P, 2, D], BF16)
         proto_signed = keep.tile([P, CHUNKS, PROTOS], F32)
         proto_sums = keep.tile([P, PROTOS], F32)
-        feat_sums = keep.tile([P, TILES], F32)
 
         nc.vector.memset(planes[:].rearrange("q w n -> q (w n)").bitcast(I32), 0)
         nc.vector.memset(bias_rows[:], 0.0)
@@ -98,10 +98,8 @@ def tile_prototypelearnerv4_pa_t_kernel(
         with ExitStack() as front:
             loads = front.enter_context(tc.tile_pool(name="loads", bufs=2))
             work = front.enter_context(tc.tile_pool(name="work", bufs=2))
-            flips = front.enter_context(tc.psum_pool(name="flips", bufs=3))
+            flips = front.enter_context(tc.psum_pool(name="flips", bufs=4))
             products = front.enter_context(tc.psum_pool(name="products", bufs=4))
-            columns = front.enter_context(tc.psum_pool(name="columns", bufs=1))
-            feat_sums_ps = columns.tile([P, CHUNKS, TILES], F32)
 
             def fetch(load):
                 rows = slice(LOAD_TILES * load, LOAD_TILES * (load + 1))
@@ -253,20 +251,6 @@ def tile_prototypelearnerv4_pa_t_kernel(
                             )
                             nc.vector.tensor_tensor(out=feat[:, c, cols], in0=x_t[:, k, :], in1=two[:], op=ADD)
 
-                    for j in range(GROUP):
-                        i = GROUP * group + j
-                        for c in range(CHUNKS):
-                            nc.tensor.matmul(
-                                out=feat_sums_ps[:, c, i : i + 1],
-                                lhsT=feat[:, c, P * i : P * (i + 1)],
-                                rhs=ones[:, 0:1],
-                                start=True,
-                                stop=True,
-                            )
-            nc.vector.tensor_reduce(
-                out=feat_sums[:], in_=feat_sums_ps[:].rearrange("b c i -> b i c"), axis=mybir.AxisListType.X, op=ADD
-            )
-
         with ExitStack() as distances:
             starts = distances.enter_context(tc.tile_pool(name="starts", bufs=10))
             runs = distances.enter_context(tc.tile_pool(name="runs", bufs=10))
@@ -275,7 +259,27 @@ def tile_prototypelearnerv4_pa_t_kernel(
             distances.enter_context(tc.manual_schedule())
 
             def chains_of(p):
+                if p % LONG_EVERY == 0:
+                    return ((0,), (1,), (2, 3))
                 return ((0,), (1,), (2,), (3,))
+
+            def fill_lanes(pieces):
+                lanes = []
+                for h in range(BLOCK_TILES // BANK_TILES):
+                    bank = banks.tile([P, BANK_TILES, P], F32, tag="lanes_%d" % h)
+                    for q in range(BANK_TILES):
+                        j = BANK_TILES * h + q
+                        for n, piece in enumerate(pieces):
+                            nc.tensor.matmul(
+                                out=bank[:, q, :],
+                                lhsT=piece[:, P * j : P * (j + 1)],
+                                rhs=ident_f[:],
+                                start=(n == 0),
+                                stop=(n == len(pieces) - 1),
+                                is_transpose=True,
+                            )
+                    lanes.append(bank)
+                return lanes
 
             def add_lanes(sums, waiting):
                 for p, lanes in waiting:
@@ -290,13 +294,16 @@ def tile_prototypelearnerv4_pa_t_kernel(
             def finish(block, sums):
                 result = results.tile([P, BLOCK_TILES, PROTOS], F32, tag="result")
                 for j in range(BLOCK_TILES):
-                    i = BLOCK_TILES * block + j
                     nc.scalar.activation(
-                        out=sums[:, j, :], in_=sums[:, j, :], func=IDENTITY, bias=feat_sums[:, i : i + 1], scale=-2.0
+                        out=sums[:, j, 0:PROTOS],
+                        in_=sums[:, j, 0:PROTOS],
+                        func=IDENTITY,
+                        bias=sums[:, j, PROTOS : PROTOS + 1],
+                        scale=-2.0,
                     )
                 nc.vector.tensor_tensor(
                     out=result[:],
-                    in0=sums[:],
+                    in0=sums[:, :, 0:PROTOS],
                     in1=proto_sums[:].unsqueeze(1).to_broadcast([P, BLOCK_TILES, PROTOS]),
                     op=ADD,
                 )
@@ -305,8 +312,8 @@ def tile_prototypelearnerv4_pa_t_kernel(
             previous = None
             for block in range(TILES // BLOCK_TILES):
                 block_cols = slice(BLOCK_COLS * block, BLOCK_COLS * (block + 1))
-                sums = results.tile([P, BLOCK_TILES, PROTOS], F32, tag="sums")
-                waiting = []
+                sums = results.tile([P, BLOCK_TILES, PROTOS + 1], F32, tag="sums")
+                waiting = [(PROTOS, fill_lanes([feat[:, c, block_cols] for c in range(CHUNKS)]))]
                 for first_p in range(0, PROTOS, ROUND):
                     round_protos = range(first_p, first_p + ROUND)
                     live = {}
@@ -343,23 +350,7 @@ def tile_prototypelearnerv4_pa_t_kernel(
                                 live[(p, chain)] = run
                     filled = []
                     for p in round_protos:
-                        chains = chains_of(p)
-                        lanes = []
-                        for h in range(BLOCK_TILES // BANK_TILES):
-                            bank = banks.tile([P, BANK_TILES, P], F32, tag="lanes_%d" % h)
-                            for q in range(BANK_TILES):
-                                j = BANK_TILES * h + q
-                                for chain in chains:
-                                    nc.tensor.matmul(
-                                        out=bank[:, q, :],
-                                        lhsT=live[(p, chain)][:, P * j : P * (j + 1)],
-                                        rhs=ident_f[:],
-                                        start=(chain == chains[0]),
-                                        stop=(chain == chains[-1]),
-                                        is_transpose=True,
-                                    )
-                            lanes.append(bank)
-                        filled.append((p, lanes))
+                        filled.append((p, fill_lanes([live[(p, chain)] for chain in chains_of(p)])))
                     add_lanes(sums, waiting)
                     waiting = filled
                     if previous is not None and first_p >= LAG:

@@ -97,7 +97,7 @@ def tile_prototypelearnerv4_pa_t_kernel(
 
         with ExitStack() as front:
             loads = front.enter_context(tc.tile_pool(name="loads", bufs=2))
-            work = front.enter_context(tc.tile_pool(name="work", bufs=2))
+            work = front.enter_context(tc.tile_pool(name="work", bufs=3))
             flips = front.enter_context(tc.psum_pool(name="flips", bufs=4))
             products = front.enter_context(tc.psum_pool(name="products", bufs=4))
 
@@ -252,8 +252,8 @@ def tile_prototypelearnerv4_pa_t_kernel(
                             nc.vector.tensor_tensor(out=feat[:, c, cols], in0=x_t[:, k, :], in1=two[:], op=ADD)
 
         with ExitStack() as distances:
-            starts = distances.enter_context(tc.tile_pool(name="starts", bufs=10))
-            runs = distances.enter_context(tc.tile_pool(name="runs", bufs=10))
+            starts = distances.enter_context(tc.tile_pool(name="starts", bufs=3 * ROUND * SCALAR_CHUNKS))
+            runs = distances.enter_context(tc.tile_pool(name="runs", bufs=3 * ROUND * (CHUNKS - SCALAR_CHUNKS)))
             results = distances.enter_context(tc.tile_pool(name="results", bufs=2))
             banks = distances.enter_context(tc.psum_pool(name="banks", bufs=2 * ROUND))
             distances.enter_context(tc.manual_schedule())
@@ -281,8 +281,8 @@ def tile_prototypelearnerv4_pa_t_kernel(
                     lanes.append(bank)
                 return lanes
 
-            def add_lanes(sums, waiting):
-                for p, lanes in waiting:
+            def add_lanes(waiting):
+                for sums, p, lanes in waiting:
                     for h in range(BLOCK_TILES // BANK_TILES):
                         nc.vector.tensor_reduce(
                             out=sums[:, BANK_TILES * h : BANK_TILES * (h + 1), p],
@@ -309,53 +309,72 @@ def tile_prototypelearnerv4_pa_t_kernel(
                 )
                 nc.sync.dma_start(out=out_rows[:, BLOCK_TILES * block : BLOCK_TILES * (block + 1), :], in_=result[:])
 
+            def prepare(block, first_p):
+                block_cols = slice(BLOCK_COLS * block, BLOCK_COLS * (block + 1))
+                round_protos = range(first_p, first_p + ROUND)
+                live = {}
+                for p in round_protos:
+                    for chain in chains_of(p):
+                        c = chain[0]
+                        if c < SCALAR_CHUNKS:
+                            run = starts.tile([P, BLOCK_COLS], F32, tag="start")
+                            nc.scalar.activation(
+                                out=run[:], in_=feat[:, c, block_cols], func=RELU, bias=proto_signed[:, c, p : p + 1]
+                            )
+                        else:
+                            run = runs.tile([P, BLOCK_COLS], F32, tag="run")
+                            nc.vector.tensor_scalar(
+                                out=run[:],
+                                in0=feat[:, c, block_cols],
+                                scalar1=proto_signed[:, c, p : p + 1],
+                                scalar2=None,
+                                op0=MAX,
+                            )
+                        live[(p, chain)] = run
+                for p in round_protos:
+                    for chain in chains_of(p):
+                        for c in chain[1:]:
+                            run = runs.tile([P, BLOCK_COLS], F32, tag="run")
+                            nc.vector.scalar_tensor_tensor(
+                                out=run[:],
+                                in0=feat[:, c, block_cols],
+                                scalar=proto_signed[:, c, p : p + 1],
+                                in1=live[(p, chain)][:],
+                                op0=MAX,
+                                op1=ADD,
+                            )
+                            live[(p, chain)] = run
+                return [(p, [live[(p, chain)] for chain in chains_of(p)]) for p in round_protos]
+
+            def round_after(block, first_p):
+                if first_p + ROUND < PROTOS:
+                    return block, first_p + ROUND
+                if block + 1 < TILES // BLOCK_TILES:
+                    return block + 1, 0
+                return None
+
+            prepared = prepare(0, 0)
+            waiting = []
             previous = None
             for block in range(TILES // BLOCK_TILES):
                 block_cols = slice(BLOCK_COLS * block, BLOCK_COLS * (block + 1))
                 sums = results.tile([P, BLOCK_TILES, PROTOS + 1], F32, tag="sums")
-                waiting = [(PROTOS, fill_lanes([feat[:, c, block_cols] for c in range(CHUNKS)]))]
+                filled = [(sums, PROTOS, fill_lanes([feat[:, c, block_cols] for c in range(CHUNKS)]))]
+                add_lanes(waiting)
+                waiting = filled
                 for first_p in range(0, PROTOS, ROUND):
-                    round_protos = range(first_p, first_p + ROUND)
-                    live = {}
-                    for p in round_protos:
-                        for chain in chains_of(p):
-                            c = chain[0]
-                            if c < SCALAR_CHUNKS:
-                                run = starts.tile([P, BLOCK_COLS], F32, tag="start")
-                                nc.scalar.activation(
-                                    out=run[:], in_=feat[:, c, block_cols], func=RELU, bias=proto_signed[:, c, p : p + 1]
-                                )
-                            else:
-                                run = runs.tile([P, BLOCK_COLS], F32, tag="run")
-                                nc.vector.tensor_scalar(
-                                    out=run[:],
-                                    in0=feat[:, c, block_cols],
-                                    scalar1=proto_signed[:, c, p : p + 1],
-                                    scalar2=None,
-                                    op0=MAX,
-                                )
-                            live[(p, chain)] = run
-                    for p in round_protos:
-                        for chain in chains_of(p):
-                            for c in chain[1:]:
-                                run = runs.tile([P, BLOCK_COLS], F32, tag="run")
-                                nc.vector.scalar_tensor_tensor(
-                                    out=run[:],
-                                    in0=feat[:, c, block_cols],
-                                    scalar=proto_signed[:, c, p : p + 1],
-                                    in1=live[(p, chain)][:],
-                                    op0=MAX,
-                                    op1=ADD,
-                                )
-                                live[(p, chain)] = run
+                    current = prepared
+                    following = round_after(block, first_p)
+                    if following is not None:
+                        prepared = prepare(*following)
                     filled = []
-                    for p in round_protos:
-                        filled.append((p, fill_lanes([live[(p, chain)] for chain in chains_of(p)])))
-                    add_lanes(sums, waiting)
+                    for p, pieces in current:
+                        filled.append((sums, p, fill_lanes(pieces)))
+                    add_lanes(waiting)
                     waiting = filled
                     if previous is not None and first_p >= LAG:
                         finish(*previous)
                         previous = None
-                add_lanes(sums, waiting)
                 previous = (block, sums)
+            add_lanes(waiting)
             finish(*previous)

@@ -12,6 +12,7 @@ FP8X4 = mybir.dt.float8_e4m3fn_x4
 FP4X4 = mybir.dt.float4_e2m1fn_x4
 ADD = mybir.AluOpType.add
 MAX = mybir.AluOpType.max
+MIN = mybir.AluOpType.min
 MULT = mybir.AluOpType.mult
 RELU = mybir.ActivationFunctionType.Relu
 IDENTITY = mybir.ActivationFunctionType.Identity
@@ -30,10 +31,14 @@ BLOCK_TILES = 8
 BLOCK_COLS = BLOCK_TILES * P
 ROUND = 2
 SCALAR_CHUNKS = 2
-LONG_EVERY = 4
+LONG_EVERY = 2
+FLOAT32_MAX = 3.4028234663852886e38
 BANK_TILES = 4
-LAG = 4
+LAG = 2 * ROUND
+WEIGHTS = 3
 A_W, W_U2, W_U3 = 0, 1, 2
+QUADRANT = 32
+QUADRANT_SCALES = 4
 
 FLOPS = 3 * 2 * BATCH * D * D + 3 * BATCH * PROTOS * D
 
@@ -76,8 +81,8 @@ def tile_prototypelearnerv4_pa_t_kernel(
     with ExitStack() as whole:
         keep = whole.enter_context(tc.tile_pool(name="keep", bufs=1))
         feat = keep.tile([P, CHUNKS, BATCH], F32)
-        words = keep.tile([P, 3, 2 * D], U8, align_bytes=64)
-        planes = keep.tile([P, 3, D], U8, align_bytes=64)
+        words = keep.tile([P, WEIGHTS, 2 * D], U8, align_bytes=64)
+        planes = keep.tile([P, WEIGHTS, D], U8, align_bytes=64)
         ident_bf = keep.tile([P, P], BF16)
         ident_f = keep.tile([P, P], F32)
         ones = keep.tile([P, P], F32)
@@ -117,10 +122,10 @@ def tile_prototypelearnerv4_pa_t_kernel(
             for w, w_words, w_scales in given:
                 nc.sync.dma_start(out=words[:, w, :].bitcast(I32), in_=w_words[0].bitcast(I32))
             for w, w_words, w_scales in given:
-                for quad in range(4):
+                for quad in range(P // QUADRANT):
                     nc.sync.dma_start(
-                        out=planes[32 * quad : 32 * quad + 4, w, :].bitcast(I32),
-                        in_=w_scales[0, 4 * quad : 4 * quad + 4, :].bitcast(I32),
+                        out=planes[QUADRANT * quad : QUADRANT * quad + QUADRANT_SCALES, w, :].bitcast(I32),
+                        in_=w_scales[0, QUADRANT_SCALES * quad : QUADRANT_SCALES * (quad + 1), :].bitcast(I32),
                     )
             nc.scalar.dma_start(out=bu2_all[:], in_=bu2.partition_broadcast(P))
             nc.scalar.dma_start(out=bias_rows[0:CHUNKS, :], in_=bu3.rearrange("(c q) -> c q", q=P))
@@ -208,16 +213,16 @@ def tile_prototypelearnerv4_pa_t_kernel(
                     flip_bf16(nc, flips, ident_bf, lambda j, t: pre_u2[:, j, t, :], u2_grouped, relu=True)
                     u2_codes, u2_scales = quantise(nc, work, u2_grouped, "u2")
 
-                    for pair in range(CHUNKS // 2):
+                    for chunk_pair in range(CHUNKS // 2):
                         x_t = flips.tile([P, 2, GROUP_COLS], BF16, tag="flip")
-                        for k in range(2):
-                            c = 2 * pair + k
+                        for side in range(2):
+                            c = 2 * chunk_pair + side
                             for j in range(GROUP):
                                 nc.tensor.transpose(
-                                    x_t[:, k, P * j : P * (j + 1)], xs[:, first + j, P * c : P * (c + 1)], ident_bf[:]
+                                    x_t[:, side, P * j : P * (j + 1)], xs[:, first + j, P * c : P * (c + 1)], ident_bf[:]
                                 )
-                        for k in range(2):
-                            c = 2 * pair + k
+                        for side in range(2):
+                            c = 2 * chunk_pair + side
                             up = products.tile([P, GROUP_COLS], F32, tag="product")
                             nc.tensor.matmul_mx(
                                 out=up[:],
@@ -249,29 +254,30 @@ def tile_prototypelearnerv4_pa_t_kernel(
                                 op0=ADD,
                                 op1=ADD,
                             )
-                            nc.vector.tensor_tensor(out=feat[:, c, cols], in0=x_t[:, k, :], in1=two[:], op=ADD)
+                            nc.vector.tensor_tensor(out=feat[:, c, cols], in0=x_t[:, side, :], in1=two[:], op=ADD)
 
         with ExitStack() as distances:
             starts = distances.enter_context(tc.tile_pool(name="starts", bufs=3 * ROUND * SCALAR_CHUNKS))
             runs = distances.enter_context(tc.tile_pool(name="runs", bufs=3 * ROUND * (CHUNKS - SCALAR_CHUNKS)))
+            thirds = distances.enter_context(tc.tile_pool(name="thirds", bufs=3 * ROUND // LONG_EVERY))
             results = distances.enter_context(tc.tile_pool(name="results", bufs=2))
             banks = distances.enter_context(tc.psum_pool(name="banks", bufs=2 * ROUND))
             distances.enter_context(tc.manual_schedule())
 
             def chains_of(p):
                 if p % LONG_EVERY == 0:
-                    return ((0,), (1,), (2, 3))
+                    return ((0,), (1,), (3, 2))
                 return ((0,), (1,), (2,), (3,))
 
             def fill_lanes(pieces):
                 lanes = []
                 for h in range(BLOCK_TILES // BANK_TILES):
                     bank = banks.tile([P, BANK_TILES, P], F32, tag="lanes_%d" % h)
-                    for q in range(BANK_TILES):
-                        j = BANK_TILES * h + q
+                    for unit in range(BANK_TILES):
+                        j = BANK_TILES * h + unit
                         for n, piece in enumerate(pieces):
                             nc.tensor.matmul(
-                                out=bank[:, q, :],
+                                out=bank[:, unit, :],
                                 lhsT=piece[:, P * j : P * (j + 1)],
                                 rhs=ident_f[:],
                                 start=(n == 0),
@@ -282,10 +288,10 @@ def tile_prototypelearnerv4_pa_t_kernel(
                 return lanes
 
             def add_lanes(waiting):
-                for sums, p, lanes in waiting:
+                for sums, column, lanes in waiting:
                     for h in range(BLOCK_TILES // BANK_TILES):
                         nc.vector.tensor_reduce(
-                            out=sums[:, BANK_TILES * h : BANK_TILES * (h + 1), p],
+                            out=sums[:, BANK_TILES * h : BANK_TILES * (h + 1), column],
                             in_=lanes[h][:],
                             axis=mybir.AxisListType.X,
                             op=ADD,
@@ -320,6 +326,16 @@ def tile_prototypelearnerv4_pa_t_kernel(
                             run = starts.tile([P, BLOCK_COLS], F32, tag="start")
                             nc.scalar.activation(
                                 out=run[:], in_=feat[:, c, block_cols], func=RELU, bias=proto_signed[:, c, p : p + 1]
+                            )
+                        elif len(chain) > 1:
+                            run = thirds.tile([P, BLOCK_COLS], F32, tag="third")
+                            nc.gpsimd.tensor_scalar(
+                                out=run[:],
+                                in0=feat[:, c, block_cols],
+                                scalar1=FLOAT32_MAX,
+                                scalar2=proto_signed[:, c, p : p + 1],
+                                op0=MIN,
+                                op1=MAX,
                             )
                         else:
                             run = runs.tile([P, BLOCK_COLS], F32, tag="run")

@@ -12,60 +12,32 @@ FP8X4 = mybir.dt.float8_e4m3fn_x4
 FP4X4 = mybir.dt.float4_e2m1fn_x4
 ADD = mybir.AluOpType.add
 MAX = mybir.AluOpType.max
-MIN = mybir.AluOpType.min
 MULT = mybir.AluOpType.mult
 RELU = mybir.ActivationFunctionType.Relu
-IDENTITY = mybir.ActivationFunctionType.Identity
 
 P = 128
 PACK = 4
 BATCH = 4096
 D = 512
-CHUNKS = D // P
 PROTOS = 200
 TILES = BATCH // P
-GROUP = 4
-GROUP_COLS = GROUP * P
-LOAD_TILES = 8
-BLOCK_TILES = 8
-BLOCK_COLS = BLOCK_TILES * P
-ROUND = 2
-SCALAR_CHUNKS = 2
-LONG_EVERY = 2
-FLOAT32_MAX = 3.4028234663852886e38
-BANK_TILES = 4
-LAG = 2 * ROUND
+FAMILIES = 4
+LANES = P // FAMILIES
+CHUNKS = D // LANES
+UNITS = TILES // FAMILIES
+COLS = UNITS * P
+GROUP_COLS = FAMILIES * P
+BANK_UNITS = 4
+BANKS = UNITS // BANK_UNITS
 WEIGHTS = 3
 A_W, W_U2, W_U3 = 0, 1, 2
 QUADRANT = 32
 QUADRANT_SCALES = 4
 
+SHARES = ((7, 5, 4), (8, 4, 4))
+SCALAR_ALWAYS = min(share[0] for share in SHARES)
+
 FLOPS = 3 * 2 * BATCH * D * D + 3 * BATCH * PROTOS * D
-
-
-def flip_bf16(nc, psum, ident, source, grouped, relu):
-    for pair in range(GROUP // 2):
-        flipped = psum.tile([P, PACK, 2 * P], BF16, tag="flip")
-        for j in range(2):
-            for t in range(PACK):
-                nc.tensor.transpose(flipped[:, t, P * j : P * (j + 1)], source(2 * pair + j, t), ident[:])
-        dst = grouped[:, 2 * P * pair : 2 * P * (pair + 1), :]
-        src = flipped[:].rearrange("q t b -> q b t")
-        if relu:
-            nc.scalar.activation(out=dst, in_=src, func=RELU)
-        else:
-            nc.scalar.copy(out=dst, in_=src)
-
-
-def quantise(nc, pool, grouped, name):
-    codes = pool.tile([P, GROUP_COLS], U32, tag="codes_" + name, align_bytes=64)
-    scales = pool.tile([P, GROUP_COLS], U8, tag="scales_" + name, align_bytes=64)
-    nc.vector.quantize_mx(
-        out=codes[:].bitcast(FP8X4),
-        scales=scales[:],
-        in_=grouped[:].rearrange("q b t -> q (b t)"),
-    )
-    return codes, scales
 
 
 def tile_prototypelearnerv4_pa_t_kernel(
@@ -80,45 +52,53 @@ def tile_prototypelearnerv4_pa_t_kernel(
 
     with ExitStack() as whole:
         keep = whole.enter_context(tc.tile_pool(name="keep", bufs=1))
-        feat = keep.tile([P, CHUNKS, BATCH], F32)
-        words = keep.tile([P, WEIGHTS, 2 * D], U8, align_bytes=64)
-        planes = keep.tile([P, WEIGHTS, D], U8, align_bytes=64)
-        ident_bf = keep.tile([P, P], BF16)
+        feat = keep.tile([P, CHUNKS, COLS], F32)
         ident_f = keep.tile([P, P], F32)
-        ones = keep.tile([P, P], F32)
-        bu2_all = keep.tile([P, D], BF16)
-        bias_rows = keep.tile([P, P], BF16)
-        bias_cols = keep.tile([P, 2 * CHUNKS], F32)
-        proto_rows = keep.tile([P, 2, D], BF16)
         proto_signed = keep.tile([P, CHUNKS, PROTOS], F32)
-        proto_sums = keep.tile([P, PROTOS], F32)
-
-        nc.vector.memset(planes[:].rearrange("q w n -> q (w n)").bitcast(I32), 0)
-        nc.vector.memset(bias_rows[:], 0.0)
-        nc.vector.memset(proto_rows[:], 0.0)
-        nc.vector.memset(ones[:], 1.0)
-        make_identity(nc, ident_bf[:])
-        make_identity(nc, ident_f[:])
+        bracket = keep.tile([P, PROTOS], F32)
+        feat_sums = keep.tile([P, TILES], F32)
 
         with ExitStack() as front:
+            once = front.enter_context(tc.tile_pool(name="once", bufs=1))
             loads = front.enter_context(tc.tile_pool(name="loads", bufs=2))
-            work = front.enter_context(tc.tile_pool(name="work", bufs=3))
+            x_loads = front.enter_context(tc.tile_pool(name="x_loads", bufs=5))
+            work = front.enter_context(tc.tile_pool(name="work", bufs=2))
+            operands = front.enter_context(tc.tile_pool(name="operands", bufs=3))
             flips = front.enter_context(tc.psum_pool(name="flips", bufs=4))
             products = front.enter_context(tc.psum_pool(name="products", bufs=4))
 
-            def fetch(load):
-                rows = slice(LOAD_TILES * load, LOAD_TILES * (load + 1))
-                hu = loads.tile([P, LOAD_TILES, D], BF16, tag="hu")
-                hs = loads.tile([P, LOAD_TILES, D], BF16, tag="hs")
-                xs = loads.tile([P, LOAD_TILES, D], BF16, tag="xs")
+            words = once.tile([P, WEIGHTS, 2 * D], U8, align_bytes=64)
+            planes = once.tile([P, WEIGHTS, D], U8, align_bytes=64)
+            u2_words = once.tile([P, 2 * D], U8, align_bytes=64)
+            u2_planes = once.tile([P, D], U8, align_bytes=64)
+            ident_bf = once.tile([P, P], BF16)
+            ones = once.tile([P, P], F32)
+            bu2_cols = once.tile([P, PACK], BF16)
+            bias_rows = once.tile([P, FAMILIES, LANES], BF16)
+            bias_cols = once.tile([P, 2 * CHUNKS], F32)
+            proto_rows = once.tile([P, 2, D], BF16)
+            proto_wide = once.tile([P, 2, CHUNKS, FAMILIES, LANES], BF16)
+
+            def fetch(u):
+                rows = slice(FAMILIES * u, FAMILIES * (u + 1))
+                hu = loads.tile([P, FAMILIES, D], BF16, tag="hu")
+                hs = loads.tile([P, FAMILIES, D], BF16, tag="hs")
+                xs = x_loads.tile([P, FAMILIES, D], BF16, tag="xs")
                 nc.sync.dma_start(out=hu[:], in_=h_up_rows[:, rows, :])
                 nc.sync.dma_start(out=hs[:], in_=h_skip_rows[:, rows, :])
                 nc.sync.dma_start(out=xs[:], in_=x_rows[:, rows, :])
                 return hu, hs, xs
 
-            fetched = fetch(0)
+            fetched = {0: fetch(0)}
 
-            given = ((A_W, aW_words, aW_scales), (W_U2, Wu2_words, Wu2_scales), (W_U3, Wu3_words, Wu3_scales))
+            nc.vector.memset(planes[:].rearrange("q w n -> q (w n)").bitcast(I32), 0)
+            nc.gpsimd.memset(bias_rows[:], 0.0)
+            nc.gpsimd.memset(proto_rows[:], 0.0)
+            nc.gpsimd.memset(ones[:], 1.0)
+            make_identity(nc, ident_bf[:])
+            make_identity(nc, ident_f[:])
+
+            given = ((W_U2, Wu2_words, Wu2_scales), (W_U3, Wu3_words, Wu3_scales), (A_W, aW_words, aW_scales))
             for w, w_words, w_scales in given:
                 nc.sync.dma_start(out=words[:, w, :].bitcast(I32), in_=w_words[0].bitcast(I32))
             for w, w_words, w_scales in given:
@@ -127,270 +107,314 @@ def tile_prototypelearnerv4_pa_t_kernel(
                         out=planes[QUADRANT * quad : QUADRANT * quad + QUADRANT_SCALES, w, :].bitcast(I32),
                         in_=w_scales[0, QUADRANT_SCALES * quad : QUADRANT_SCALES * (quad + 1), :].bitcast(I32),
                     )
-            nc.scalar.dma_start(out=bu2_all[:], in_=bu2.partition_broadcast(P))
-            nc.scalar.dma_start(out=bias_rows[0:CHUNKS, :], in_=bu3.rearrange("(c q) -> c q", q=P))
-            nc.scalar.dma_start(out=bias_rows[CHUNKS : 2 * CHUNKS, :], in_=ab.rearrange("(c q) -> c q", q=P))
+            nc.scalar.dma_start(out=bu2_cols[:], in_=bu2.rearrange("(q t) -> q t", t=PACK))
+            for h in range(FAMILIES):
+                nc.scalar.dma_start(out=bias_rows[0:CHUNKS, h, :], in_=bu3.rearrange("(c i) -> c i", i=LANES))
+                nc.scalar.dma_start(out=bias_rows[CHUNKS : 2 * CHUNKS, h, :], in_=ab.rearrange("(c i) -> c i", i=LANES))
             nc.scalar.dma_start(out=proto_rows[:, 0, :], in_=protos[0:P, :])
             nc.scalar.dma_start(out=proto_rows[0 : PROTOS - P, 1, :], in_=protos[P:PROTOS, :])
 
-            bias_t = flips.tile([P, P], BF16, tag="flip")
-            nc.tensor.transpose(bias_t[:], bias_rows[:], ident_bf[:])
-            nc.vector.tensor_copy(out=bias_cols[:], in_=bias_t[:, 0 : 2 * CHUNKS])
-            proto_ps = flips.tile([P, CHUNKS, 2 * P], BF16, tag="flip")
-            for c in range(CHUNKS):
-                for half in range(2):
-                    nc.tensor.transpose(
-                        proto_ps[:, c, P * half : P * (half + 1)],
-                        proto_rows[:, half, P * c : P * (c + 1)],
-                        ident_bf[:],
-                    )
-            nc.vector.tensor_copy(out=proto_signed[:], in_=proto_ps[:, :, 0:PROTOS])
-            nc.vector.tensor_scalar(
-                out=proto_signed[:, 0:SCALAR_CHUNKS, :],
-                in0=proto_ps[:, 0:SCALAR_CHUNKS, 0:PROTOS],
-                scalar1=-1.0,
-                scalar2=None,
-                op0=MULT,
+            nc.vector.tensor_copy(
+                out=u2_words[:].rearrange("k (t q b) -> k q t b", t=PACK, b=2),
+                in_=words[:, W_U2, :].rearrange("k (q t b) -> k q t b", t=PACK, b=2),
             )
-            proto_sums_ps = flips.tile([P, PROTOS], F32, tag="flip")
-            for c in range(CHUNKS):
-                nc.tensor.matmul(
-                    out=proto_sums_ps[:], lhsT=ones[:], rhs=proto_signed[:, c, :], start=(c == 0), stop=(c == CHUNKS - 1)
-                )
-            nc.vector.tensor_copy(out=proto_sums[:], in_=proto_sums_ps[:])
+            nc.vector.tensor_copy(
+                out=u2_planes[:].rearrange("k (t q) -> k q t", t=PACK),
+                in_=planes[:, W_U2, :].rearrange("k (q t) -> k q t", t=PACK),
+            )
 
-            for load in range(TILES // LOAD_TILES):
-                hu, hs, xs = fetched
-                if load + 1 < TILES // LOAD_TILES:
-                    fetched = fetch(load + 1)
-
-                for part in range(LOAD_TILES // GROUP):
-                    first = GROUP * part
-                    group = (LOAD_TILES // GROUP) * load + part
-                    cols = slice(GROUP_COLS * group, GROUP_COLS * (group + 1))
-
-                    z = work.tile([P, GROUP, D], BF16, tag="z")
-                    nc.vector.tensor_tensor(
-                        out=z[:], in0=hu[:, first : first + GROUP, :], in1=hs[:, first : first + GROUP, :], op=ADD
+            def sum_and_flip(u):
+                hu, hs, xs = fetched[u]
+                z = work.tile([P, FAMILIES, D], BF16, tag="z")
+                nc.vector.tensor_tensor(out=z[:], in0=hu[:], in1=hs[:], op=ADD)
+                z_grouped = work.tile([P, GROUP_COLS, PACK], BF16, tag="z_grouped", align_bytes=64)
+                for pair in range(FAMILIES // 2):
+                    flipped = flips.tile([P, PACK, 2 * P], BF16, tag="flip")
+                    for j in range(2):
+                        for t in range(PACK):
+                            nc.tensor.transpose(
+                                flipped[:, t, P * j : P * (j + 1)], z[:, 2 * pair + j, t:D:PACK], ident_bf[:]
+                            )
+                    nc.scalar.copy(
+                        out=z_grouped[:, 2 * P * pair : 2 * P * (pair + 1), :], in_=flipped[:].rearrange("q t b -> q b t")
                     )
-                    z_grouped = work.tile([P, GROUP_COLS, PACK], BF16, tag="z_grouped", align_bytes=64)
-                    flip_bf16(nc, flips, ident_bf, lambda j, t: z[:, j, t:D:PACK], z_grouped, relu=False)
-                    z_codes, z_scales = quantise(nc, work, z_grouped, "z")
+                x_grouped = work.tile([P, GROUP_COLS, PACK], BF16, tag="x_grouped", align_bytes=64)
+                x_pairs = x_grouped[:].rearrange("q b t -> q (b t)").bitcast(F32).rearrange("q (b v) -> q b v", v=2)
+                for pair in range(FAMILIES // 2):
+                    flipped = flips.tile([P, 2, 2 * P], F32, tag="flip")
+                    for j in range(2):
+                        x_words = xs[:, 2 * pair + j, :].bitcast(F32)
+                        for v in range(2):
+                            nc.tensor.transpose(flipped[:, v, P * j : P * (j + 1)], x_words[:, v : D // 2 : 2], ident_f[:])
+                    nc.scalar.copy(
+                        out=x_pairs[:, 2 * P * pair : 2 * P * (pair + 1), :], in_=flipped[:].rearrange("q v b -> q b v")
+                    )
+                return quantise(z_grouped, "z"), quantise(x_grouped, "x")
 
-                    x_grouped = work.tile([P, GROUP_COLS, PACK], BF16, tag="x_grouped", align_bytes=64)
-                    x_pairs = x_grouped[:].rearrange("q b t -> q (b t)").bitcast(F32).rearrange("q (b u) -> q b u", u=2)
-                    for pair in range(GROUP // 2):
-                        flipped = flips.tile([P, 2, 2 * P], F32, tag="flip")
-                        for j in range(2):
-                            x_words = xs[:, first + 2 * pair + j, :].bitcast(F32)
-                            for u in range(2):
-                                nc.tensor.transpose(flipped[:, u, P * j : P * (j + 1)], x_words[:, u : D // 2 : 2], ident_f[:])
-                        nc.scalar.copy(
-                            out=x_pairs[:, 2 * P * pair : 2 * P * (pair + 1), :],
-                            in_=flipped[:].rearrange("q u b -> q b u"),
-                        )
-                    x_codes, x_scales = quantise(nc, work, x_grouped, "x")
+            def quantise(grouped, name):
+                codes = operands.tile([P, GROUP_COLS], U32, tag="codes_" + name, align_bytes=64)
+                scales = operands.tile([P, GROUP_COLS], U8, tag="scales_" + name, align_bytes=64)
+                nc.vector.quantize_mx(
+                    out=codes[:].bitcast(FP8X4), scales=scales[:], in_=grouped[:].rearrange("q b t -> q (b t)")
+                )
+                return codes, scales
 
-                    pre_u2 = work.tile([P, GROUP, PACK, P], BF16, tag="pre_u2")
-                    for j in range(GROUP):
-                        product = products.tile([P, D], F32, tag="product")
+            def make_u2(z_quantised):
+                z_codes, z_scales = z_quantised
+                u2_grouped = work.tile([P, GROUP_COLS, PACK], BF16, tag="u2_grouped", align_bytes=64)
+                for h in range(FAMILIES):
+                    rows = slice(P * h, P * (h + 1))
+                    product = products.tile([P, PACK, P], F32, tag="product")
+                    for t in range(PACK):
                         nc.tensor.matmul_mx(
-                            out=product[:],
-                            lhsT=z_codes[:, P * j : P * (j + 1)].bitcast(FP8X4),
-                            lhsT_scale=z_scales[:, P * j : P * (j + 1)],
-                            rhs=words[:, W_U2, :].bitcast(FP4X4),
-                            rhs_scale=planes[:, W_U2, :],
+                            out=product[:, t, :],
+                            lhsT=u2_words[:, 2 * P * t : 2 * P * (t + 1)].bitcast(FP4X4),
+                            lhsT_scale=u2_planes[:, P * t : P * (t + 1)],
+                            rhs=z_codes[:, rows].bitcast(FP8X4),
+                            rhs_scale=z_scales[:, rows],
                             start=True,
                             stop=True,
                         )
-                        nc.vector.tensor_tensor(
-                            out=pre_u2[:, j, :, :],
-                            in0=product[:].rearrange("b (q t) -> b t q", t=PACK),
-                            in1=bu2_all[:].rearrange("b (q t) -> b t q", t=PACK),
-                            op=ADD,
-                        )
-                    u2_grouped = work.tile([P, GROUP_COLS, PACK], BF16, tag="u2_grouped", align_bytes=64)
-                    flip_bf16(nc, flips, ident_bf, lambda j, t: pre_u2[:, j, t, :], u2_grouped, relu=True)
-                    u2_codes, u2_scales = quantise(nc, work, u2_grouped, "u2")
+                    nc.vector.tensor_tensor(
+                        out=u2_grouped[:, rows, :],
+                        in0=product[:].rearrange("q t b -> q b t"),
+                        in1=bu2_cols[:].unsqueeze(1).to_broadcast([P, P, PACK]),
+                        op=ADD,
+                    )
+                flat = u2_grouped[:].rearrange("q b t -> q (b t)")
+                nc.vector.tensor_scalar(out=flat, in0=flat, scalar1=0.0, scalar2=None, op0=MAX)
+                return quantise(u2_grouped, "u2")
 
-                    for chunk_pair in range(CHUNKS // 2):
-                        x_t = flips.tile([P, 2, GROUP_COLS], BF16, tag="flip")
-                        for side in range(2):
-                            c = 2 * chunk_pair + side
-                            for j in range(GROUP):
-                                nc.tensor.transpose(
-                                    x_t[:, side, P * j : P * (j + 1)], xs[:, first + j, P * c : P * (c + 1)], ident_bf[:]
-                                )
-                        for side in range(2):
-                            c = 2 * chunk_pair + side
-                            up = products.tile([P, GROUP_COLS], F32, tag="product")
-                            nc.tensor.matmul_mx(
-                                out=up[:],
-                                lhsT=words[:, W_U3, 2 * P * c : 2 * P * (c + 1)].bitcast(FP4X4),
-                                lhsT_scale=planes[:, W_U3, P * c : P * (c + 1)],
-                                rhs=u2_codes[:].bitcast(FP8X4),
-                                rhs_scale=u2_scales[:],
-                                start=True,
-                                stop=True,
+            def make_streams(u, u2_quantised, x_quantised):
+                u2_codes, u2_scales = u2_quantised
+                x_codes, x_scales = x_quantised
+                xs = fetched[u][2]
+                up_rows = work.tile([P, CHUNKS, FAMILIES, LANES], F32, tag="up_rows")
+                adapted = work.tile([P, CHUNKS, FAMILIES, LANES], F32, tag="adapted")
+                for h in range(FAMILIES):
+                    rows = slice(P * h, P * (h + 1))
+                    up = products.tile([P, D], F32, tag="product")
+                    nc.tensor.matmul_mx(
+                        out=up[:],
+                        lhsT=u2_codes[:, rows].bitcast(FP8X4),
+                        lhsT_scale=u2_scales[:, rows],
+                        rhs=words[:, W_U3, :].bitcast(FP4X4),
+                        rhs_scale=planes[:, W_U3, :],
+                        start=True,
+                        stop=True,
+                    )
+                    adapter = products.tile([P, D], F32, tag="product")
+                    nc.tensor.matmul_mx(
+                        out=adapter[:],
+                        lhsT=x_codes[:, rows].bitcast(FP8X4),
+                        lhsT_scale=x_scales[:, rows],
+                        rhs=words[:, A_W, :].bitcast(FP4X4),
+                        rhs_scale=planes[:, A_W, :],
+                        start=True,
+                        stop=True,
+                    )
+                    nc.scalar.copy(out=up_rows[:, :, h, :], in_=up[:].rearrange("r (c i) -> r c i", i=LANES))
+                    nc.vector.tensor_tensor(
+                        out=adapted[:, :, h, :],
+                        in0=adapter[:].rearrange("r (c i) -> r c i", i=LANES),
+                        in1=xs[:, h, :].rearrange("r (c i) -> r c i", i=LANES),
+                        op=ADD,
+                    )
+                return up_rows, adapted
+
+            def make_features(u, streams):
+                up_rows, adapted = streams
+                cols = slice(P * u, P * (u + 1))
+                for first in range(0, CHUNKS, BANK_UNITS):
+                    up_t = flips.tile([P, BANK_UNITS, P], F32, tag="flip")
+                    adapted_t = flips.tile([P, BANK_UNITS, P], F32, tag="flip")
+                    for n in range(BANK_UNITS):
+                        c = first + n
+                        nc.tensor.transpose(up_t[:, n, :], up_rows[:, c, :, :].rearrange("r h i -> r (h i)"), ident_f[:])
+                        nc.tensor.transpose(adapted_t[:, n, :], adapted[:, c, :, :].rearrange("r h i -> r (h i)"), ident_f[:])
+                    u3 = work.tile([P, BANK_UNITS, P], F32, tag="u3")
+                    for n in range(BANK_UNITS):
+                        c = first + n
+                        nc.scalar.activation(out=u3[:, n, :], in_=up_t[:, n, :], func=RELU, bias=bias_cols[:, c : c + 1])
+                        nc.vector.scalar_tensor_tensor(
+                            out=feat[:, c, cols],
+                            in0=adapted_t[:, n, :],
+                            scalar=bias_cols[:, CHUNKS + c : CHUNKS + c + 1],
+                            in1=u3[:, n, :],
+                            op0=ADD,
+                            op1=ADD,
+                        )
+
+            def add_features(first_unit):
+                bank = flips.tile([P, BANK_UNITS, P], F32, tag="flip")
+                for unit in range(BANK_UNITS):
+                    cols = slice(P * (first_unit + unit), P * (first_unit + unit + 1))
+                    for c in range(CHUNKS):
+                        nc.tensor.matmul(
+                            out=bank[:, unit, :],
+                            lhsT=feat[:, c, cols],
+                            rhs=ident_f[:],
+                            start=(c == 0),
+                            stop=(c == CHUNKS - 1),
+                            is_transpose=True,
+                        )
+                nc.vector.tensor_reduce(
+                    out=feat_sums[:, FAMILIES * first_unit : FAMILIES * (first_unit + BANK_UNITS)],
+                    in_=bank[:].rearrange("r u (h i) -> r (u h) i", i=LANES),
+                    axis=mybir.AxisListType.X,
+                    op=ADD,
+                )
+
+            def small_tables():
+                bias_t = flips.tile([P, P], BF16, tag="flip")
+                nc.tensor.transpose(bias_t[:], bias_rows[:].rearrange("c h i -> c (h i)"), ident_bf[:])
+                nc.vector.tensor_copy(out=bias_cols[:], in_=bias_t[:, 0 : 2 * CHUNKS])
+                for h in range(FAMILIES):
+                    nc.vector.tensor_copy(
+                        out=proto_wide[:, :, :, h, :], in_=proto_rows[:].rearrange("p s (c i) -> p s c i", i=LANES)
+                    )
+                for first in range(0, CHUNKS, BANK_UNITS):
+                    chunk_t = flips.tile([P, BANK_UNITS, 2 * P], BF16, tag="flip")
+                    for n in range(BANK_UNITS):
+                        for half in range(2):
+                            nc.tensor.transpose(
+                                chunk_t[:, n, P * half : P * (half + 1)],
+                                proto_wide[:, half, first + n, :, :].rearrange("p h i -> p (h i)"),
+                                ident_bf[:],
                             )
-                            adapter = products.tile([P, GROUP_COLS], F32, tag="product")
-                            nc.tensor.matmul_mx(
-                                out=adapter[:],
-                                lhsT=words[:, A_W, 2 * P * c : 2 * P * (c + 1)].bitcast(FP4X4),
-                                lhsT_scale=planes[:, A_W, P * c : P * (c + 1)],
-                                rhs=x_codes[:].bitcast(FP8X4),
-                                rhs_scale=x_scales[:],
-                                start=True,
-                                stop=True,
-                            )
-                            u3 = work.tile([P, GROUP_COLS], F32, tag="u3")
-                            nc.scalar.activation(out=u3[:], in_=up[:], func=RELU, bias=bias_cols[:, c : c + 1])
-                            two = work.tile([P, GROUP_COLS], F32, tag="two")
-                            nc.vector.scalar_tensor_tensor(
-                                out=two[:],
-                                in0=adapter[:],
-                                scalar=bias_cols[:, CHUNKS + c : CHUNKS + c + 1],
-                                in1=u3[:],
-                                op0=ADD,
-                                op1=ADD,
-                            )
-                            nc.vector.tensor_tensor(out=feat[:, c, cols], in0=x_t[:, side, :], in1=two[:], op=ADD)
+                    nc.vector.tensor_copy(out=proto_signed[:, first : first + BANK_UNITS, :], in_=chunk_t[:, :, 0:PROTOS])
+                for parity in range(len(SHARES)):
+                    mine = proto_signed[:, 0 : SHARES[parity][0], parity : PROTOS : len(SHARES)]
+                    nc.vector.tensor_scalar(out=mine, in0=mine, scalar1=-1.0, scalar2=None, op0=MULT)
+                bracket_ps = flips.tile([P, PROTOS], F32, tag="flip")
+                for c in range(CHUNKS):
+                    nc.tensor.matmul(
+                        out=bracket_ps[:],
+                        lhsT=ones[:],
+                        rhs=proto_signed[:, c, :],
+                        start=(c == 0),
+                        stop=(c == CHUNKS - 1),
+                    )
+                nc.vector.tensor_scalar(
+                    out=bracket[:], in0=bracket_ps[:], scalar1=-1.0 / (2 * LANES * FAMILIES), scalar2=None, op0=MULT
+                )
+
+            quantised = {}
+            second = {}
+            streams = {}
+            for step in range(UNITS + 3):
+                if step + 1 < UNITS:
+                    fetched[step + 1] = fetch(step + 1)
+                if 0 <= step - 3:
+                    make_features(step - 3, streams[step - 3])
+                if 0 <= step - 2 < UNITS:
+                    streams[step - 2] = make_streams(step - 2, second[step - 2], quantised[step - 2][1])
+                if 0 <= step - 1 < UNITS:
+                    second[step - 1] = make_u2(quantised[step - 1][0])
+                if step < UNITS:
+                    quantised[step] = sum_and_flip(step)
+                if step == 0:
+                    small_tables()
+                if step - 3 == BANK_UNITS - 1 or step - 3 == UNITS - 1:
+                    add_features(step - 3 - (BANK_UNITS - 1))
 
         with ExitStack() as distances:
-            starts = distances.enter_context(tc.tile_pool(name="starts", bufs=3 * ROUND * SCALAR_CHUNKS))
-            runs = distances.enter_context(tc.tile_pool(name="runs", bufs=3 * ROUND * (CHUNKS - SCALAR_CHUNKS)))
-            thirds = distances.enter_context(tc.tile_pool(name="thirds", bufs=3 * ROUND // LONG_EVERY))
-            results = distances.enter_context(tc.tile_pool(name="results", bufs=2))
-            banks = distances.enter_context(tc.psum_pool(name="banks", bufs=2 * ROUND))
+            scalar_pieces = distances.enter_context(tc.tile_pool(name="scalar_pieces", bufs=18))
+            vector_pieces = distances.enter_context(tc.tile_pool(name="vector_pieces", bufs=12))
+            results = distances.enter_context(tc.tile_pool(name="results", bufs=1))
+            banks = distances.enter_context(tc.psum_pool(name="banks", bufs=4))
+            sums = results.tile([P, TILES, PROTOS], F32)
             distances.enter_context(tc.manual_schedule())
 
-            def chains_of(p):
-                if p % LONG_EVERY == 0:
-                    return ((0,), (1,), (3, 2))
-                return ((0,), (1,), (2,), (3,))
+            def prepare(p):
+                scalars, begun, added = SHARES[p % len(SHARES)]
+                pieces = []
+                for c in range(scalars):
+                    piece = scalar_pieces.tile([P, COLS], F32, tag="scalar_piece")
+                    nc.scalar.activation(out=piece[:], in_=feat[:, c, :], func=RELU, bias=proto_signed[:, c, p : p + 1])
+                    pieces.append(piece)
+                mine = []
+                for n in range(begun):
+                    c = scalars + n
+                    piece = vector_pieces.tile([P, COLS], F32, tag="vector_piece")
+                    if n == 0:
+                        nc.vector.tensor_scalar(
+                            out=piece[:],
+                            in0=feat[:, c, :],
+                            scalar1=proto_signed[:, c, p : p + 1],
+                            scalar2=bracket[:, p : p + 1],
+                            op0=MAX,
+                            op1=ADD,
+                        )
+                    else:
+                        nc.vector.tensor_scalar(
+                            out=piece[:], in0=feat[:, c, :], scalar1=proto_signed[:, c, p : p + 1], scalar2=None, op0=MAX
+                        )
+                    mine.append(piece)
+                for n in range(added):
+                    c = scalars + begun + n
+                    nc.vector.scalar_tensor_tensor(
+                        out=mine[n][:],
+                        in0=feat[:, c, :],
+                        scalar=proto_signed[:, c, p : p + 1],
+                        in1=mine[n][:],
+                        op0=MAX,
+                        op1=ADD,
+                    )
+                return pieces + mine
 
             def fill_lanes(pieces):
                 lanes = []
-                for h in range(BLOCK_TILES // BANK_TILES):
-                    bank = banks.tile([P, BANK_TILES, P], F32, tag="lanes_%d" % h)
-                    for unit in range(BANK_TILES):
-                        j = BANK_TILES * h + unit
-                        for n, piece in enumerate(pieces):
+                for n in range(BANKS):
+                    bank = banks.tile([P, BANK_UNITS, P], F32, tag="lanes_%d" % n)
+                    for unit in range(BANK_UNITS):
+                        u = BANK_UNITS * n + unit
+                        for k, piece in enumerate(pieces):
                             nc.tensor.matmul(
                                 out=bank[:, unit, :],
-                                lhsT=piece[:, P * j : P * (j + 1)],
+                                lhsT=piece[:, P * u : P * (u + 1)],
                                 rhs=ident_f[:],
-                                start=(n == 0),
-                                stop=(n == len(pieces) - 1),
+                                start=(k == 0),
+                                stop=(k == len(pieces) - 1),
                                 is_transpose=True,
                             )
                     lanes.append(bank)
                 return lanes
 
-            def add_lanes(waiting):
-                for sums, column, lanes in waiting:
-                    for h in range(BLOCK_TILES // BANK_TILES):
-                        nc.vector.tensor_reduce(
-                            out=sums[:, BANK_TILES * h : BANK_TILES * (h + 1), column],
-                            in_=lanes[h][:],
-                            axis=mybir.AxisListType.X,
-                            op=ADD,
-                        )
-
-            def finish(block, sums):
-                result = results.tile([P, BLOCK_TILES, PROTOS], F32, tag="result")
-                for j in range(BLOCK_TILES):
-                    nc.scalar.activation(
-                        out=sums[:, j, 0:PROTOS],
-                        in_=sums[:, j, 0:PROTOS],
-                        func=IDENTITY,
-                        bias=sums[:, j, PROTOS : PROTOS + 1],
-                        scale=-2.0,
+            def add_lanes(p, lanes):
+                tiles = FAMILIES * BANK_UNITS
+                for n in range(BANKS):
+                    nc.vector.tensor_reduce(
+                        out=sums[:, tiles * n : tiles * (n + 1), p],
+                        in_=lanes[n][:].rearrange("r u (h i) -> r (u h) i", i=LANES),
+                        axis=mybir.AxisListType.X,
+                        op=ADD,
                     )
-                nc.vector.tensor_tensor(
-                    out=result[:],
-                    in0=sums[:, :, 0:PROTOS],
-                    in1=proto_sums[:].unsqueeze(1).to_broadcast([P, BLOCK_TILES, PROTOS]),
-                    op=ADD,
+
+            def finish(first_p, end_p):
+                mine = sums[:, :, first_p:end_p]
+                nc.vector.scalar_tensor_tensor(
+                    out=mine,
+                    in0=mine,
+                    scalar=-2.0,
+                    in1=feat_sums[:].unsqueeze(2).to_broadcast([P, TILES, end_p - first_p]),
+                    op0=MULT,
+                    op1=ADD,
                 )
-                nc.sync.dma_start(out=out_rows[:, BLOCK_TILES * block : BLOCK_TILES * (block + 1), :], in_=result[:])
+                nc.sync.dma_start(out=out_rows[:, :, first_p:end_p], in_=mine)
 
-            def prepare(block, first_p):
-                block_cols = slice(BLOCK_COLS * block, BLOCK_COLS * (block + 1))
-                round_protos = range(first_p, first_p + ROUND)
-                live = {}
-                for p in round_protos:
-                    for chain in chains_of(p):
-                        c = chain[0]
-                        if c < SCALAR_CHUNKS:
-                            run = starts.tile([P, BLOCK_COLS], F32, tag="start")
-                            nc.scalar.activation(
-                                out=run[:], in_=feat[:, c, block_cols], func=RELU, bias=proto_signed[:, c, p : p + 1]
-                            )
-                        elif len(chain) > 1:
-                            run = thirds.tile([P, BLOCK_COLS], F32, tag="third")
-                            nc.gpsimd.tensor_scalar(
-                                out=run[:],
-                                in0=feat[:, c, block_cols],
-                                scalar1=FLOAT32_MAX,
-                                scalar2=proto_signed[:, c, p : p + 1],
-                                op0=MIN,
-                                op1=MAX,
-                            )
-                        else:
-                            run = runs.tile([P, BLOCK_COLS], F32, tag="run")
-                            nc.vector.tensor_scalar(
-                                out=run[:],
-                                in0=feat[:, c, block_cols],
-                                scalar1=proto_signed[:, c, p : p + 1],
-                                scalar2=None,
-                                op0=MAX,
-                            )
-                        live[(p, chain)] = run
-                for p in round_protos:
-                    for chain in chains_of(p):
-                        for c in chain[1:]:
-                            run = runs.tile([P, BLOCK_COLS], F32, tag="run")
-                            nc.vector.scalar_tensor_tensor(
-                                out=run[:],
-                                in0=feat[:, c, block_cols],
-                                scalar=proto_signed[:, c, p : p + 1],
-                                in1=live[(p, chain)][:],
-                                op0=MAX,
-                                op1=ADD,
-                            )
-                            live[(p, chain)] = run
-                return [(p, [live[(p, chain)] for chain in chains_of(p)]) for p in round_protos]
-
-            def round_after(block, first_p):
-                if first_p + ROUND < PROTOS:
-                    return block, first_p + ROUND
-                if block + 1 < TILES // BLOCK_TILES:
-                    return block + 1, 0
-                return None
-
-            prepared = prepare(0, 0)
-            waiting = []
-            previous = None
-            for block in range(TILES // BLOCK_TILES):
-                block_cols = slice(BLOCK_COLS * block, BLOCK_COLS * (block + 1))
-                sums = results.tile([P, BLOCK_TILES, PROTOS + 1], F32, tag="sums")
-                filled = [(sums, PROTOS, fill_lanes([feat[:, c, block_cols] for c in range(CHUNKS)]))]
-                add_lanes(waiting)
-                waiting = filled
-                for first_p in range(0, PROTOS, ROUND):
-                    current = prepared
-                    following = round_after(block, first_p)
-                    if following is not None:
-                        prepared = prepare(*following)
-                    filled = []
-                    for p, pieces in current:
-                        filled.append((sums, p, fill_lanes(pieces)))
-                    add_lanes(waiting)
-                    waiting = filled
-                    if previous is not None and first_p >= LAG:
-                        finish(*previous)
-                        previous = None
-                previous = (block, sums)
-            add_lanes(waiting)
-            finish(*previous)
+            HALF = 104
+            pieces = prepare(0)
+            waiting = None
+            for p in range(PROTOS):
+                current = pieces
+                if p + 1 < PROTOS:
+                    pieces = prepare(p + 1)
+                lanes = fill_lanes(current)
+                if waiting is not None:
+                    add_lanes(*waiting)
+                waiting = (p, lanes)
+                if p == HALF + 1:
+                    finish(0, HALF)
+            add_lanes(*waiting)
+            finish(HALF, PROTOS)

@@ -322,7 +322,8 @@ def tile_prototypelearnerv4_pa_t_kernel(
             scalar_pieces = distances.enter_context(tc.tile_pool(name="scalar_pieces", bufs=18))
             vector_pieces = distances.enter_context(tc.tile_pool(name="vector_pieces", bufs=12))
             results = distances.enter_context(tc.tile_pool(name="results", bufs=1))
-            banks = distances.enter_context(tc.psum_pool(name="banks", bufs=4))
+            banks = distances.enter_context(tc.psum_pool(name="banks", bufs=3))
+            spare = distances.enter_context(tc.psum_pool(name="spare", bufs=1))
             sums = results.tile([P, TILES, PROTOS], F32)
             distances.enter_context(tc.manual_schedule())
 
@@ -363,7 +364,12 @@ def tile_prototypelearnerv4_pa_t_kernel(
                     )
                 return pieces + mine
 
-            def fill_lanes(pieces):
+            def keep_warm(count):
+                product = spare.tile([P, P], F32, tag="spare")
+                for n in range(count):
+                    nc.tensor.matmul(out=product[:], lhsT=ident_f[:], rhs=ident_f[:], start=True, stop=True)
+
+            def fill_lanes(pieces, warm):
                 lanes = []
                 for n in range(BANKS):
                     bank = banks.tile([P, BANK_UNITS, P], F32, tag="lanes_%d" % n)
@@ -378,6 +384,8 @@ def tile_prototypelearnerv4_pa_t_kernel(
                                 stop=(k == len(pieces) - 1),
                                 is_transpose=True,
                             )
+                        if u == 0 and warm > 0:
+                            keep_warm(warm)
                     lanes.append(bank)
                 return lanes
 
@@ -403,6 +411,9 @@ def tile_prototypelearnerv4_pa_t_kernel(
                 )
                 nc.sync.dma_start(out=out_rows[:, :, first_p:end_p], in_=mine)
 
+            WARM_EVERY = 8
+            WARM_FIRST = 6
+            WARM_LATER = 3
             HALF = 104
             pieces = prepare(0)
             waiting = None
@@ -410,7 +421,7 @@ def tile_prototypelearnerv4_pa_t_kernel(
                 current = pieces
                 if p + 1 < PROTOS:
                     pieces = prepare(p + 1)
-                lanes = fill_lanes(current)
+                lanes = fill_lanes(current, WARM_FIRST if p == 0 else WARM_LATER if p % WARM_EVERY == 0 else 0)
                 if waiting is not None:
                     add_lanes(*waiting)
                 waiting = (p, lanes)

@@ -21,21 +21,24 @@ BATCH = 4096
 D = 512
 PROTOS = 200
 TILES = BATCH // P
-FAMILIES = 4
+FAMILIES = 8
 LANES = P // FAMILIES
 CHUNKS = D // LANES
 UNITS = TILES // FAMILIES
 COLS = UNITS * P
-GROUP_COLS = FAMILIES * P
-BANK_UNITS = 4
-BANKS = UNITS // BANK_UNITS
+GROUP = 4
+GROUP_COLS = GROUP * P
+GROUPS = TILES // GROUP
+HALVES = FAMILIES // GROUP
+BANK_SQUARES = 4
 WEIGHTS = 3
 A_W, W_U2, W_U3 = 0, 1, 2
 QUADRANT = 32
 QUADRANT_SCALES = 4
 
-SHARES = ((7, 5, 4), (8, 4, 4))
-SCALAR_ALWAYS = min(share[0] for share in SHARES)
+SCALARS = 14
+BEGUN = 11
+ADDED = CHUNKS - SCALARS - BEGUN
 
 FLOPS = 3 * 2 * BATCH * D * D + 3 * BATCH * PROTOS * D
 
@@ -54,15 +57,17 @@ def tile_prototypelearnerv4_pa_t_kernel(
         keep = whole.enter_context(tc.tile_pool(name="keep", bufs=1))
         feat = keep.tile([P, CHUNKS, COLS], F32)
         ident_f = keep.tile([P, P], F32)
-        proto_signed = keep.tile([P, CHUNKS, PROTOS], F32)
+        proto_signed = keep.tile([P, CHUNKS, PROTOS], BF16)
+        proto_first = keep.tile([P, PROTOS], F32)
         bracket = keep.tile([P, PROTOS], F32)
         feat_sums = keep.tile([P, TILES], F32)
 
         with ExitStack() as front:
             once = front.enter_context(tc.tile_pool(name="once", bufs=1))
             loads = front.enter_context(tc.tile_pool(name="loads", bufs=2))
-            x_loads = front.enter_context(tc.tile_pool(name="x_loads", bufs=5))
+            x_loads = front.enter_context(tc.tile_pool(name="x_loads", bufs=4))
             work = front.enter_context(tc.tile_pool(name="work", bufs=2))
+            grouped_tiles = front.enter_context(tc.tile_pool(name="grouped_tiles", bufs=3))
             operands = front.enter_context(tc.tile_pool(name="operands", bufs=3))
             flips = front.enter_context(tc.psum_pool(name="flips", bufs=4))
             products = front.enter_context(tc.psum_pool(name="products", bufs=4))
@@ -72,18 +77,17 @@ def tile_prototypelearnerv4_pa_t_kernel(
             u2_words = once.tile([P, 2 * D], U8, align_bytes=64)
             u2_planes = once.tile([P, D], U8, align_bytes=64)
             ident_bf = once.tile([P, P], BF16)
-            ones = once.tile([P, P], F32)
+            ones = once.tile([P, P], BF16)
             bu2_cols = once.tile([P, PACK], BF16)
             bias_rows = once.tile([P, FAMILIES, LANES], BF16)
             bias_cols = once.tile([P, 2 * CHUNKS], F32)
             proto_rows = once.tile([P, 2, D], BF16)
-            proto_wide = once.tile([P, 2, CHUNKS, FAMILIES, LANES], BF16)
 
-            def fetch(u):
-                rows = slice(FAMILIES * u, FAMILIES * (u + 1))
-                hu = loads.tile([P, FAMILIES, D], BF16, tag="hu")
-                hs = loads.tile([P, FAMILIES, D], BF16, tag="hs")
-                xs = x_loads.tile([P, FAMILIES, D], BF16, tag="xs")
+            def fetch(g):
+                rows = slice(GROUP * g, GROUP * (g + 1))
+                hu = loads.tile([P, GROUP, D], BF16, tag="hu")
+                hs = loads.tile([P, GROUP, D], BF16, tag="hs")
+                xs = x_loads.tile([P, GROUP, D], BF16, tag="xs")
                 nc.sync.dma_start(out=hu[:], in_=h_up_rows[:, rows, :])
                 nc.sync.dma_start(out=hs[:], in_=h_skip_rows[:, rows, :])
                 nc.sync.dma_start(out=xs[:], in_=x_rows[:, rows, :])
@@ -123,12 +127,12 @@ def tile_prototypelearnerv4_pa_t_kernel(
                 in_=planes[:, W_U2, :].rearrange("k (q t) -> k q t", t=PACK),
             )
 
-            def sum_and_flip(u):
-                hu, hs, xs = fetched[u]
-                z = work.tile([P, FAMILIES, D], BF16, tag="z")
+            def sum_and_flip(g):
+                hu, hs, xs = fetched[g]
+                z = work.tile([P, GROUP, D], BF16, tag="z")
                 nc.vector.tensor_tensor(out=z[:], in0=hu[:], in1=hs[:], op=ADD)
-                z_grouped = work.tile([P, GROUP_COLS, PACK], BF16, tag="z_grouped", align_bytes=64)
-                for pair in range(FAMILIES // 2):
+                z_grouped = grouped_tiles.tile([P, GROUP_COLS, PACK], BF16, tag="grouped", align_bytes=64)
+                for pair in range(GROUP // 2):
                     flipped = flips.tile([P, PACK, 2 * P], BF16, tag="flip")
                     for j in range(2):
                         for t in range(PACK):
@@ -138,9 +142,9 @@ def tile_prototypelearnerv4_pa_t_kernel(
                     nc.scalar.copy(
                         out=z_grouped[:, 2 * P * pair : 2 * P * (pair + 1), :], in_=flipped[:].rearrange("q t b -> q b t")
                     )
-                x_grouped = work.tile([P, GROUP_COLS, PACK], BF16, tag="x_grouped", align_bytes=64)
+                x_grouped = grouped_tiles.tile([P, GROUP_COLS, PACK], BF16, tag="grouped", align_bytes=64)
                 x_pairs = x_grouped[:].rearrange("q b t -> q (b t)").bitcast(F32).rearrange("q (b v) -> q b v", v=2)
-                for pair in range(FAMILIES // 2):
+                for pair in range(GROUP // 2):
                     flipped = flips.tile([P, 2, 2 * P], F32, tag="flip")
                     for j in range(2):
                         x_words = xs[:, 2 * pair + j, :].bitcast(F32)
@@ -161,9 +165,9 @@ def tile_prototypelearnerv4_pa_t_kernel(
 
             def make_u2(z_quantised):
                 z_codes, z_scales = z_quantised
-                u2_grouped = work.tile([P, GROUP_COLS, PACK], BF16, tag="u2_grouped", align_bytes=64)
-                for h in range(FAMILIES):
-                    rows = slice(P * h, P * (h + 1))
+                u2_grouped = grouped_tiles.tile([P, GROUP_COLS, PACK], BF16, tag="grouped", align_bytes=64)
+                for j in range(GROUP):
+                    rows = slice(P * j, P * (j + 1))
                     product = products.tile([P, PACK, P], F32, tag="product")
                     for t in range(PACK):
                         nc.tensor.matmul_mx(
@@ -185,14 +189,14 @@ def tile_prototypelearnerv4_pa_t_kernel(
                 nc.vector.tensor_scalar(out=flat, in0=flat, scalar1=0.0, scalar2=None, op0=MAX)
                 return quantise(u2_grouped, "u2")
 
-            def make_streams(u, u2_quantised, x_quantised):
+            def make_streams(g, u2_quantised, x_quantised, streams):
                 u2_codes, u2_scales = u2_quantised
                 x_codes, x_scales = x_quantised
-                xs = fetched[u][2]
-                up_rows = work.tile([P, CHUNKS, FAMILIES, LANES], F32, tag="up_rows")
-                adapted = work.tile([P, CHUNKS, FAMILIES, LANES], F32, tag="adapted")
-                for h in range(FAMILIES):
-                    rows = slice(P * h, P * (h + 1))
+                xs = fetched[g][2]
+                up_rows, adapted = streams
+                for j in range(GROUP):
+                    h = GROUP * (g % HALVES) + j
+                    rows = slice(P * j, P * (j + 1))
                     up = products.tile([P, D], F32, tag="product")
                     nc.tensor.matmul_mx(
                         out=up[:],
@@ -217,23 +221,27 @@ def tile_prototypelearnerv4_pa_t_kernel(
                     nc.vector.tensor_tensor(
                         out=adapted[:, :, h, :],
                         in0=adapter[:].rearrange("r (c i) -> r c i", i=LANES),
-                        in1=xs[:, h, :].rearrange("r (c i) -> r c i", i=LANES),
+                        in1=xs[:, j, :].rearrange("r (c i) -> r c i", i=LANES),
                         op=ADD,
                     )
+
+            def stream_tiles():
+                up_rows = work.tile([P, CHUNKS, FAMILIES, LANES], F32, tag="up_rows")
+                adapted = work.tile([P, CHUNKS, FAMILIES, LANES], F32, tag="adapted")
                 return up_rows, adapted
 
             def make_features(u, streams):
                 up_rows, adapted = streams
                 cols = slice(P * u, P * (u + 1))
-                for first in range(0, CHUNKS, BANK_UNITS):
-                    up_t = flips.tile([P, BANK_UNITS, P], F32, tag="flip")
-                    adapted_t = flips.tile([P, BANK_UNITS, P], F32, tag="flip")
-                    for n in range(BANK_UNITS):
+                for first in range(0, CHUNKS, BANK_SQUARES):
+                    up_t = flips.tile([P, BANK_SQUARES, P], F32, tag="flip")
+                    adapted_t = flips.tile([P, BANK_SQUARES, P], F32, tag="flip")
+                    for n in range(BANK_SQUARES):
                         c = first + n
                         nc.tensor.transpose(up_t[:, n, :], up_rows[:, c, :, :].rearrange("r h i -> r (h i)"), ident_f[:])
                         nc.tensor.transpose(adapted_t[:, n, :], adapted[:, c, :, :].rearrange("r h i -> r (h i)"), ident_f[:])
-                    u3 = work.tile([P, BANK_UNITS, P], F32, tag="u3")
-                    for n in range(BANK_UNITS):
+                    u3 = work.tile([P, BANK_SQUARES, P], F32, tag="u3")
+                    for n in range(BANK_SQUARES):
                         c = first + n
                         nc.scalar.activation(out=u3[:, n, :], in_=up_t[:, n, :], func=RELU, bias=bias_cols[:, c : c + 1])
                         nc.vector.scalar_tensor_tensor(
@@ -245,22 +253,20 @@ def tile_prototypelearnerv4_pa_t_kernel(
                             op1=ADD,
                         )
 
-            def add_features(first_unit):
-                bank = flips.tile([P, BANK_UNITS, P], F32, tag="flip")
-                for unit in range(BANK_UNITS):
-                    cols = slice(P * (first_unit + unit), P * (first_unit + unit + 1))
-                    for c in range(CHUNKS):
-                        nc.tensor.matmul(
-                            out=bank[:, unit, :],
-                            lhsT=feat[:, c, cols],
-                            rhs=ident_f[:],
-                            start=(c == 0),
-                            stop=(c == CHUNKS - 1),
-                            is_transpose=True,
-                        )
+            def add_features(u):
+                square = flips.tile([P, P], F32, tag="flip")
+                for c in range(CHUNKS):
+                    nc.tensor.matmul(
+                        out=square[:],
+                        lhsT=feat[:, c, P * u : P * (u + 1)],
+                        rhs=ident_f[:],
+                        start=(c == 0),
+                        stop=(c == CHUNKS - 1),
+                        is_transpose=True,
+                    )
                 nc.vector.tensor_reduce(
-                    out=feat_sums[:, FAMILIES * first_unit : FAMILIES * (first_unit + BANK_UNITS)],
-                    in_=bank[:].rearrange("r u (h i) -> r (u h) i", i=LANES),
+                    out=feat_sums[:, FAMILIES * u : FAMILIES * (u + 1)],
+                    in_=square[:].rearrange("r (h i) -> r h i", i=LANES),
                     axis=mybir.AxisListType.X,
                     op=ADD,
                 )
@@ -269,23 +275,23 @@ def tile_prototypelearnerv4_pa_t_kernel(
                 bias_t = flips.tile([P, P], BF16, tag="flip")
                 nc.tensor.transpose(bias_t[:], bias_rows[:].rearrange("c h i -> c (h i)"), ident_bf[:])
                 nc.vector.tensor_copy(out=bias_cols[:], in_=bias_t[:, 0 : 2 * CHUNKS])
-                for h in range(FAMILIES):
-                    nc.vector.tensor_copy(
-                        out=proto_wide[:, :, :, h, :], in_=proto_rows[:].rearrange("p s (c i) -> p s c i", i=LANES)
-                    )
-                for first in range(0, CHUNKS, BANK_UNITS):
-                    chunk_t = flips.tile([P, BANK_UNITS, 2 * P], BF16, tag="flip")
-                    for n in range(BANK_UNITS):
+                for first in range(0, CHUNKS, BANK_SQUARES):
+                    proto_wide = work.tile([P, 2, BANK_SQUARES, FAMILIES, LANES], BF16, tag="proto_wide")
+                    some = proto_rows[:, :, LANES * first : LANES * (first + BANK_SQUARES)]
+                    for h in range(FAMILIES):
+                        nc.vector.tensor_copy(out=proto_wide[:, :, :, h, :], in_=some.rearrange("p s (c i) -> p s c i", i=LANES))
+                    chunk_t = flips.tile([P, BANK_SQUARES, 2 * P], BF16, tag="flip")
+                    for n in range(BANK_SQUARES):
                         for half in range(2):
                             nc.tensor.transpose(
                                 chunk_t[:, n, P * half : P * (half + 1)],
-                                proto_wide[:, half, first + n, :, :].rearrange("p h i -> p (h i)"),
+                                proto_wide[:, half, n, :, :].rearrange("p h i -> p (h i)"),
                                 ident_bf[:],
                             )
-                    nc.vector.tensor_copy(out=proto_signed[:, first : first + BANK_UNITS, :], in_=chunk_t[:, :, 0:PROTOS])
-                for parity in range(len(SHARES)):
-                    mine = proto_signed[:, 0 : SHARES[parity][0], parity : PROTOS : len(SHARES)]
-                    nc.vector.tensor_scalar(out=mine, in0=mine, scalar1=-1.0, scalar2=None, op0=MULT)
+                    nc.vector.tensor_copy(out=proto_signed[:, first : first + BANK_SQUARES, :], in_=chunk_t[:, :, 0:PROTOS])
+                mine = proto_signed[:, 0:SCALARS, :]
+                nc.vector.tensor_scalar(out=mine, in0=mine, scalar1=-1.0, scalar2=None, op0=MULT)
+                nc.vector.tensor_copy(out=proto_first[:], in_=proto_signed[:, SCALARS, :])
                 bracket_ps = flips.tile([P, PROTOS], F32, tag="flip")
                 for c in range(CHUNKS):
                     nc.tensor.matmul(
@@ -302,47 +308,50 @@ def tile_prototypelearnerv4_pa_t_kernel(
             quantised = {}
             second = {}
             streams = {}
-            for step in range(UNITS + 3):
-                if step + 1 < UNITS:
+            for step in range(GROUPS + 3):
+                if step + 1 < GROUPS:
                     fetched[step + 1] = fetch(step + 1)
-                if 0 <= step - 3:
-                    make_features(step - 3, streams[step - 3])
-                if 0 <= step - 2 < UNITS:
-                    streams[step - 2] = make_streams(step - 2, second[step - 2], quantised[step - 2][1])
-                if 0 <= step - 1 < UNITS:
+                if step >= 3 and (step - 3) % HALVES == HALVES - 1:
+                    u = (step - 3) // HALVES
+                    make_features(u, streams[u])
+                    add_features(u)
+                if 0 <= step - 2 < GROUPS:
+                    g = step - 2
+                    u = g // HALVES
+                    if g % HALVES == 0:
+                        streams[u] = stream_tiles()
+                    make_streams(g, second[g], quantised[g][1], streams[u])
+                if 0 <= step - 1 < GROUPS:
                     second[step - 1] = make_u2(quantised[step - 1][0])
-                if step < UNITS:
+                if step < GROUPS:
                     quantised[step] = sum_and_flip(step)
                 if step == 0:
                     small_tables()
-                if step - 3 == BANK_UNITS - 1 or step - 3 == UNITS - 1:
-                    add_features(step - 3 - (BANK_UNITS - 1))
 
         with ExitStack() as distances:
-            scalar_pieces = distances.enter_context(tc.tile_pool(name="scalar_pieces", bufs=18))
-            vector_pieces = distances.enter_context(tc.tile_pool(name="vector_pieces", bufs=12))
+            scalar_pieces = distances.enter_context(tc.tile_pool(name="scalar_pieces", bufs=35))
+            vector_pieces = distances.enter_context(tc.tile_pool(name="vector_pieces", bufs=27))
             results = distances.enter_context(tc.tile_pool(name="results", bufs=1))
-            banks = distances.enter_context(tc.psum_pool(name="banks", bufs=3))
+            banks = distances.enter_context(tc.psum_pool(name="banks", bufs=6))
             spare = distances.enter_context(tc.psum_pool(name="spare", bufs=1))
             sums = results.tile([P, TILES, PROTOS], F32)
             distances.enter_context(tc.manual_schedule())
 
             def prepare(p):
-                scalars, begun, added = SHARES[p % len(SHARES)]
                 pieces = []
-                for c in range(scalars):
+                for c in range(SCALARS):
                     piece = scalar_pieces.tile([P, COLS], F32, tag="scalar_piece")
                     nc.scalar.activation(out=piece[:], in_=feat[:, c, :], func=RELU, bias=proto_signed[:, c, p : p + 1])
                     pieces.append(piece)
                 mine = []
-                for n in range(begun):
-                    c = scalars + n
+                for n in range(BEGUN):
+                    c = SCALARS + n
                     piece = vector_pieces.tile([P, COLS], F32, tag="vector_piece")
                     if n == 0:
                         nc.vector.tensor_scalar(
                             out=piece[:],
                             in0=feat[:, c, :],
-                            scalar1=proto_signed[:, c, p : p + 1],
+                            scalar1=proto_first[:, p : p + 1],
                             scalar2=bracket[:, p : p + 1],
                             op0=MAX,
                             op1=ADD,
@@ -352,8 +361,8 @@ def tile_prototypelearnerv4_pa_t_kernel(
                             out=piece[:], in0=feat[:, c, :], scalar1=proto_signed[:, c, p : p + 1], scalar2=None, op0=MAX
                         )
                     mine.append(piece)
-                for n in range(added):
-                    c = scalars + begun + n
+                for n in range(ADDED):
+                    c = SCALARS + BEGUN + n
                     nc.vector.scalar_tensor_tensor(
                         out=mine[n][:],
                         in0=feat[:, c, :],
@@ -370,34 +379,28 @@ def tile_prototypelearnerv4_pa_t_kernel(
                     nc.tensor.matmul(out=product[:], lhsT=ident_f[:], rhs=ident_f[:], start=True, stop=True)
 
             def fill_lanes(pieces, warm):
-                lanes = []
-                for n in range(BANKS):
-                    bank = banks.tile([P, BANK_UNITS, P], F32, tag="lanes_%d" % n)
-                    for unit in range(BANK_UNITS):
-                        u = BANK_UNITS * n + unit
-                        for k, piece in enumerate(pieces):
-                            nc.tensor.matmul(
-                                out=bank[:, unit, :],
-                                lhsT=piece[:, P * u : P * (u + 1)],
-                                rhs=ident_f[:],
-                                start=(k == 0),
-                                stop=(k == len(pieces) - 1),
-                                is_transpose=True,
-                            )
-                        if u == 0 and warm > 0:
-                            keep_warm(warm)
-                    lanes.append(bank)
+                lanes = banks.tile([P, BANK_SQUARES, P], F32, tag="lanes")
+                for u in range(UNITS):
+                    for k, piece in enumerate(pieces):
+                        nc.tensor.matmul(
+                            out=lanes[:, u, :],
+                            lhsT=piece[:, P * u : P * (u + 1)],
+                            rhs=ident_f[:],
+                            start=(k == 0),
+                            stop=(k == len(pieces) - 1),
+                            is_transpose=True,
+                        )
+                    if u == 0 and warm > 0:
+                        keep_warm(warm)
                 return lanes
 
             def add_lanes(p, lanes):
-                tiles = FAMILIES * BANK_UNITS
-                for n in range(BANKS):
-                    nc.vector.tensor_reduce(
-                        out=sums[:, tiles * n : tiles * (n + 1), p],
-                        in_=lanes[n][:].rearrange("r u (h i) -> r (u h) i", i=LANES),
-                        axis=mybir.AxisListType.X,
-                        op=ADD,
-                    )
+                nc.vector.tensor_reduce(
+                    out=sums[:, :, p],
+                    in_=lanes[:].rearrange("r u (h i) -> r (u h) i", i=LANES),
+                    axis=mybir.AxisListType.X,
+                    op=ADD,
+                )
 
             def finish(first_p, end_p):
                 mine = sums[:, :, first_p:end_p]

@@ -29,6 +29,7 @@ COLS = UNITS * P
 GROUP = 4
 GROUP_COLS = GROUP * P
 GROUPS = TILES // GROUP
+SET = 4
 HALVES = FAMILIES // GROUP
 BANK_SQUARES = 4
 WEIGHTS = 3
@@ -329,106 +330,124 @@ def tile_prototypelearnerv4_pa_t_kernel(
                     small_tables()
 
         with ExitStack() as distances:
-            scalar_pieces = distances.enter_context(tc.tile_pool(name="scalar_pieces", bufs=35))
-            vector_pieces = distances.enter_context(tc.tile_pool(name="vector_pieces", bufs=27))
+            scalar_pieces = distances.enter_context(tc.tile_pool(name="scalar_pieces", bufs=20))
+            vector_pieces = distances.enter_context(tc.tile_pool(name="vector_pieces", bufs=20))
             results = distances.enter_context(tc.tile_pool(name="results", bufs=1))
-            banks = distances.enter_context(tc.psum_pool(name="banks", bufs=6))
-            spare = distances.enter_context(tc.psum_pool(name="spare", bufs=1))
+            banks = distances.enter_context(tc.psum_pool(name="banks", bufs=2))
             sums = results.tile([P, TILES, PROTOS], F32)
             distances.enter_context(tc.manual_schedule())
 
-            def prepare(p):
-                pieces = []
-                for c in range(SCALARS):
-                    piece = scalar_pieces.tile([P, COLS], F32, tag="scalar_piece")
-                    nc.scalar.activation(out=piece[:], in_=feat[:, c, :], func=RELU, bias=proto_signed[:, c, p : p + 1])
-                    pieces.append(piece)
-                mine = []
-                for n in range(BEGUN):
-                    c = SCALARS + n
-                    piece = vector_pieces.tile([P, COLS], F32, tag="vector_piece")
-                    if n == 0:
-                        nc.vector.tensor_scalar(
-                            out=piece[:],
-                            in0=feat[:, c, :],
-                            scalar1=proto_first[:, p : p + 1],
-                            scalar2=bracket[:, p : p + 1],
-                            op0=MAX,
-                            op1=ADD,
-                        )
-                    else:
-                        nc.vector.tensor_scalar(
-                            out=piece[:], in0=feat[:, c, :], scalar1=proto_signed[:, c, p : p + 1], scalar2=None, op0=MAX
-                        )
-                    mine.append(piece)
-                for n in range(ADDED):
-                    c = SCALARS + BEGUN + n
-                    nc.vector.scalar_tensor_tensor(
-                        out=mine[n][:],
+            def begin(p, n):
+                c = SCALARS + n
+                piece = vector_pieces.tile([P, COLS], F32, tag="vector_piece")
+                if n == 0:
+                    nc.vector.tensor_scalar(
+                        out=piece[:],
                         in0=feat[:, c, :],
-                        scalar=proto_signed[:, c, p : p + 1],
-                        in1=mine[n][:],
+                        scalar1=proto_first[:, p : p + 1],
+                        scalar2=bracket[:, p : p + 1],
                         op0=MAX,
                         op1=ADD,
                     )
-                return pieces + mine
+                else:
+                    nc.vector.tensor_scalar(
+                        out=piece[:], in0=feat[:, c, :], scalar1=proto_signed[:, c, p : p + 1], scalar2=None, op0=MAX
+                    )
+                return piece
 
-            def keep_warm(count):
-                product = spare.tile([P, P], F32, tag="spare")
-                for n in range(count):
-                    nc.tensor.matmul(out=product[:], lhsT=ident_f[:], rhs=ident_f[:], start=True, stop=True)
+            def add_chunk(p, piece, c):
+                nc.vector.scalar_tensor_tensor(
+                    out=piece[:],
+                    in0=feat[:, c, :],
+                    scalar=proto_signed[:, c, p : p + 1],
+                    in1=piece[:],
+                    op0=MAX,
+                    op1=ADD,
+                )
 
-            def fill_lanes(pieces, warm):
-                lanes = banks.tile([P, BANK_SQUARES, P], F32, tag="lanes")
-                for u in range(UNITS):
-                    for k, piece in enumerate(pieces):
+            def prepare(p):
+                scalar_made = []
+                for c in range(SCALARS):
+                    piece = scalar_pieces.tile([P, COLS], F32, tag="scalar_piece")
+                    nc.scalar.activation(out=piece[:], in_=feat[:, c, :], func=RELU, bias=proto_signed[:, c, p : p + 1])
+                    scalar_made.append(((2 * c + 1) / SCALARS, piece))
+                vector_made = []
+                added = 0
+                for n in range(BEGUN + 1):
+                    if n < BEGUN:
+                        piece = begin(p, n)
+                        vector_made.append(((2 * n + 1) / BEGUN, piece))
+                    if n > 0 and n * ADDED // BEGUN > added:
+                        add_chunk(p, vector_made[n - 1][1], SCALARS + BEGUN + added)
+                        added += 1
+                return [piece for place, piece in sorted(scalar_made + vector_made, key=lambda made: made[0])]
+
+            def transpose_pieces(pieces, lanes, slot):
+                for k, piece in enumerate(pieces):
+                    for u in range(UNITS):
                         nc.tensor.matmul(
-                            out=lanes[:, u, :],
+                            out=lanes[u][:, slot, :],
                             lhsT=piece[:, P * u : P * (u + 1)],
                             rhs=ident_f[:],
                             start=(k == 0),
                             stop=(k == len(pieces) - 1),
                             is_transpose=True,
                         )
-                    if u == 0 and warm > 0:
-                        keep_warm(warm)
-                return lanes
 
-            def add_lanes(p, lanes):
+            def keep_warm(lanes, count):
+                for n in range(count):
+                    nc.tensor.matmul(out=lanes[0][:, SET - 1, :], lhsT=ident_f[:], rhs=ident_f[:], start=True, stop=True)
+
+            def add_lanes(first_p, lanes, u):
                 nc.vector.tensor_reduce(
-                    out=sums[:, :, p],
-                    in_=lanes[:].rearrange("r u (h i) -> r (u h) i", i=LANES),
+                    out=sums[:, FAMILIES * u : FAMILIES * (u + 1), first_p : first_p + SET].rearrange("r h s -> r s h"),
+                    in_=lanes[u][:].rearrange("r s (h i) -> r s h i", i=LANES),
                     axis=mybir.AxisListType.X,
                     op=ADD,
                 )
 
-            def finish(first_p, end_p):
-                mine = sums[:, :, first_p:end_p]
+            def finish(first_p, end_p, first_tile, end_tile):
+                mine = sums[:, first_tile:end_tile, first_p:end_p]
+                row_sums = feat_sums[:, first_tile:end_tile].unsqueeze(2)
                 nc.vector.scalar_tensor_tensor(
                     out=mine,
                     in0=mine,
                     scalar=-2.0,
-                    in1=feat_sums[:].unsqueeze(2).to_broadcast([P, TILES, end_p - first_p]),
+                    in1=row_sums.to_broadcast([P, end_tile - first_tile, end_p - first_p]),
                     op0=MULT,
                     op1=ADD,
                 )
-                nc.sync.dma_start(out=out_rows[:, :, first_p:end_p], in_=mine)
 
-            WARM_EVERY = 8
+            def store(first_p, end_p):
+                nc.sync.dma_start(out=out_rows[:, :, first_p:end_p], in_=sums[:, :, first_p:end_p])
+
+            EARLY = 104
+            SLICE = 4
+            WARM_EVERY = 2
             WARM_FIRST = 6
             WARM_LATER = 3
-            HALF = 104
-            pieces = prepare(0)
-            waiting = None
+            full = None
             for p in range(PROTOS):
-                current = pieces
-                if p + 1 < PROTOS:
-                    pieces = prepare(p + 1)
-                lanes = fill_lanes(current, WARM_FIRST if p == 0 else WARM_LATER if p % WARM_EVERY == 0 else 0)
-                if waiting is not None:
-                    add_lanes(*waiting)
-                waiting = (p, lanes)
-                if p == HALF + 1:
-                    finish(0, HALF)
-            add_lanes(*waiting)
-            finish(HALF, PROTOS)
+                slot = p % SET
+                if slot == 0:
+                    lanes = []
+                    for u in range(UNITS):
+                        bank = banks.tile([P, SET, P], F32, tag="lanes_%d" % u)
+                        lanes.append(bank)
+                    if p // SET % WARM_EVERY == 0:
+                        keep_warm(lanes, WARM_FIRST if p == 0 else WARM_LATER)
+                pieces = prepare(p)
+                if full is not None:
+                    add_lanes(full[0], full[1], slot)
+                transpose_pieces(pieces, lanes, slot)
+                late = p - EARLY - SET
+                if 0 <= late < TILES // SLICE:
+                    finish(0, EARLY, SLICE * late, SLICE * (late + 1))
+                if late == TILES // SLICE:
+                    store(0, EARLY)
+                if slot == SET - 1:
+                    full = (p - slot, lanes)
+            for u in range(UNITS):
+                add_lanes(full[0], full[1], u)
+            finish(EARLY, PROTOS, 0, TILES)
+            store(EARLY, PROTOS)

@@ -68,7 +68,8 @@ def tile_prototypelearnerv4_pa_t_kernel(
             loads = front.enter_context(tc.tile_pool(name="loads", bufs=2))
             x_loads = front.enter_context(tc.tile_pool(name="x_loads", bufs=4))
             work = front.enter_context(tc.tile_pool(name="work", bufs=2))
-            grouped_tiles = front.enter_context(tc.tile_pool(name="grouped_tiles", bufs=3))
+            stream_pool = front.enter_context(tc.tile_pool(name="streams", bufs=3))
+            grouped_tiles = front.enter_context(tc.tile_pool(name="grouped_tiles", bufs=2))
             operands = front.enter_context(tc.tile_pool(name="operands", bufs=3))
             flips = front.enter_context(tc.psum_pool(name="flips", bufs=4))
             products = front.enter_context(tc.psum_pool(name="products", bufs=4))
@@ -78,7 +79,9 @@ def tile_prototypelearnerv4_pa_t_kernel(
             u2_words = once.tile([P, 2 * D], U8, align_bytes=64)
             u2_planes = once.tile([P, D], U8, align_bytes=64)
             ident_bf = once.tile([P, P], BF16)
-            ones = once.tile([P, P], BF16)
+            signs = once.tile([P, D // P, P], BF16)
+            select = once.tile([P, FAMILIES, FAMILIES, LANES], BF16)
+            proto_t = once.tile([P, D // P, 2 * P], BF16)
             bu2_cols = once.tile([P, PACK], BF16)
             bias_rows = once.tile([P, FAMILIES, LANES], BF16)
             bias_cols = once.tile([P, 2 * CHUNKS], F32)
@@ -99,9 +102,16 @@ def tile_prototypelearnerv4_pa_t_kernel(
             nc.vector.memset(planes[:].rearrange("q w n -> q (w n)").bitcast(I32), 0)
             nc.gpsimd.memset(bias_rows[:], 0.0)
             nc.gpsimd.memset(proto_rows[:], 0.0)
-            nc.gpsimd.memset(ones[:], 1.0)
             make_identity(nc, ident_bf[:])
             make_identity(nc, ident_f[:])
+            for s in range(D // P):
+                negative = min(max(SCALARS * LANES - P * s, 0), P)
+                if negative < P:
+                    nc.gpsimd.memset(signs[:, s, :], 1.0)
+                if negative > 0:
+                    nc.gpsimd.memset(signs[0:negative, s, :], -1.0)
+            for h in range(FAMILIES):
+                nc.gpsimd.tensor_copy(out=select[:, :, h, :], in_=ident_bf[:].rearrange("k (v i) -> k v i", i=LANES))
 
             given = ((W_U2, Wu2_words, Wu2_scales), (W_U3, Wu3_words, Wu3_scales), (A_W, aW_words, aW_scales))
             for w, w_words, w_scales in given:
@@ -119,20 +129,14 @@ def tile_prototypelearnerv4_pa_t_kernel(
             nc.scalar.dma_start(out=proto_rows[:, 0, :], in_=protos[0:P, :])
             nc.scalar.dma_start(out=proto_rows[0 : PROTOS - P, 1, :], in_=protos[P:PROTOS, :])
 
-            nc.vector.tensor_copy(
-                out=u2_words[:].rearrange("k (t q b) -> k q t b", t=PACK, b=2),
-                in_=words[:, W_U2, :].rearrange("k (q t b) -> k q t b", t=PACK, b=2),
-            )
-            nc.vector.tensor_copy(
-                out=u2_planes[:].rearrange("k (t q) -> k q t", t=PACK),
-                in_=planes[:, W_U2, :].rearrange("k (q t) -> k q t", t=PACK),
-            )
-
-            def sum_and_flip(g):
+            def add_up(g):
                 hu, hs, xs = fetched[g]
                 z = work.tile([P, GROUP, D], BF16, tag="z")
                 nc.vector.tensor_tensor(out=z[:], in0=hu[:], in1=hs[:], op=ADD)
-                z_grouped = grouped_tiles.tile([P, GROUP_COLS, PACK], BF16, tag="grouped", align_bytes=64)
+                return z
+
+            def flip(g, z):
+                z_grouped = grouped_tiles.tile([P, GROUP_COLS, PACK], BF16, tag="z_grouped", align_bytes=64)
                 for pair in range(GROUP // 2):
                     flipped = flips.tile([P, PACK, 2 * P], BF16, tag="flip")
                     for j in range(2):
@@ -143,7 +147,8 @@ def tile_prototypelearnerv4_pa_t_kernel(
                     nc.scalar.copy(
                         out=z_grouped[:, 2 * P * pair : 2 * P * (pair + 1), :], in_=flipped[:].rearrange("q t b -> q b t")
                     )
-                x_grouped = grouped_tiles.tile([P, GROUP_COLS, PACK], BF16, tag="grouped", align_bytes=64)
+                xs = fetched[g][2]
+                x_grouped = grouped_tiles.tile([P, GROUP_COLS, PACK], BF16, tag="x_grouped", align_bytes=64)
                 x_pairs = x_grouped[:].rearrange("q b t -> q (b t)").bitcast(F32).rearrange("q (b v) -> q b v", v=2)
                 for pair in range(GROUP // 2):
                     flipped = flips.tile([P, 2, 2 * P], F32, tag="flip")
@@ -154,7 +159,7 @@ def tile_prototypelearnerv4_pa_t_kernel(
                     nc.scalar.copy(
                         out=x_pairs[:, 2 * P * pair : 2 * P * (pair + 1), :], in_=flipped[:].rearrange("q v b -> q b v")
                     )
-                return quantise(z_grouped, "z"), quantise(x_grouped, "x")
+                return z_grouped, x_grouped
 
             def quantise(grouped, name):
                 codes = operands.tile([P, GROUP_COLS], U32, tag="codes_" + name, align_bytes=64)
@@ -166,7 +171,7 @@ def tile_prototypelearnerv4_pa_t_kernel(
 
             def make_u2(z_quantised):
                 z_codes, z_scales = z_quantised
-                u2_grouped = grouped_tiles.tile([P, GROUP_COLS, PACK], BF16, tag="grouped", align_bytes=64)
+                u2_grouped = grouped_tiles.tile([P, GROUP_COLS, PACK], BF16, tag="u2_grouped", align_bytes=64)
                 for j in range(GROUP):
                     rows = slice(P * j, P * (j + 1))
                     product = products.tile([P, PACK, P], F32, tag="product")
@@ -188,13 +193,20 @@ def tile_prototypelearnerv4_pa_t_kernel(
                     )
                 flat = u2_grouped[:].rearrange("q b t -> q (b t)")
                 nc.vector.tensor_scalar(out=flat, in0=flat, scalar1=0.0, scalar2=None, op0=MAX)
-                return quantise(u2_grouped, "u2")
+                return u2_grouped
 
-            def make_streams(g, u2_quantised, x_quantised, streams):
+            def stream_tiles():
+                tiles = []
+                for half in range(2):
+                    up_rows = stream_pool.tile([P, CHUNKS // 2, FAMILIES, LANES], F32, tag="up_rows")
+                    adapted = stream_pool.tile([P, CHUNKS // 2, FAMILIES, LANES], F32, tag="adapted")
+                    tiles.append((up_rows, adapted))
+                return tiles
+
+            def make_streams(g, u2_quantised, x_quantised, tiles):
                 u2_codes, u2_scales = u2_quantised
                 x_codes, x_scales = x_quantised
                 xs = fetched[g][2]
-                up_rows, adapted = streams
                 for j in range(GROUP):
                     h = GROUP * (g % HALVES) + j
                     rows = slice(P * j, P * (j + 1))
@@ -218,32 +230,32 @@ def tile_prototypelearnerv4_pa_t_kernel(
                         start=True,
                         stop=True,
                     )
-                    nc.scalar.copy(out=up_rows[:, :, h, :], in_=up[:].rearrange("r (c i) -> r c i", i=LANES))
-                    nc.vector.tensor_tensor(
-                        out=adapted[:, :, h, :],
-                        in0=adapter[:].rearrange("r (c i) -> r c i", i=LANES),
-                        in1=xs[:, j, :].rearrange("r (c i) -> r c i", i=LANES),
-                        op=ADD,
-                    )
+                    for half in range(2):
+                        up_rows, adapted = tiles[half]
+                        features = slice(D // 2 * half, D // 2 * (half + 1))
+                        nc.scalar.copy(out=up_rows[:, :, h, :], in_=up[:, features].rearrange("r (c i) -> r c i", i=LANES))
+                        nc.vector.tensor_tensor(
+                            out=adapted[:, :, h, :],
+                            in0=adapter[:, features].rearrange("r (c i) -> r c i", i=LANES),
+                            in1=xs[:, j, features].rearrange("r (c i) -> r c i", i=LANES),
+                            op=ADD,
+                        )
 
-            def stream_tiles():
-                up_rows = work.tile([P, CHUNKS, FAMILIES, LANES], F32, tag="up_rows")
-                adapted = work.tile([P, CHUNKS, FAMILIES, LANES], F32, tag="adapted")
-                return up_rows, adapted
-
-            def make_features(u, streams):
-                up_rows, adapted = streams
+            def make_features(u, half, tiles):
+                up_rows, adapted = tiles[half]
                 cols = slice(P * u, P * (u + 1))
-                for first in range(0, CHUNKS, BANK_SQUARES):
+                for first in range(0, CHUNKS // 2, BANK_SQUARES):
                     up_t = flips.tile([P, BANK_SQUARES, P], F32, tag="flip")
+                    for n in range(BANK_SQUARES):
+                        nc.tensor.transpose(up_t[:, n, :], up_rows[:, first + n, :, :].rearrange("r h i -> r (h i)"), ident_f[:])
                     adapted_t = flips.tile([P, BANK_SQUARES, P], F32, tag="flip")
                     for n in range(BANK_SQUARES):
-                        c = first + n
-                        nc.tensor.transpose(up_t[:, n, :], up_rows[:, c, :, :].rearrange("r h i -> r (h i)"), ident_f[:])
-                        nc.tensor.transpose(adapted_t[:, n, :], adapted[:, c, :, :].rearrange("r h i -> r (h i)"), ident_f[:])
+                        nc.tensor.transpose(
+                            adapted_t[:, n, :], adapted[:, first + n, :, :].rearrange("r h i -> r (h i)"), ident_f[:]
+                        )
                     u3 = work.tile([P, BANK_SQUARES, P], F32, tag="u3")
                     for n in range(BANK_SQUARES):
-                        c = first + n
+                        c = CHUNKS // 2 * half + first + n
                         nc.scalar.activation(out=u3[:, n, :], in_=up_t[:, n, :], func=RELU, bias=bias_cols[:, c : c + 1])
                         nc.vector.scalar_tensor_tensor(
                             out=feat[:, c, cols],
@@ -265,6 +277,9 @@ def tile_prototypelearnerv4_pa_t_kernel(
                         stop=(c == CHUNKS - 1),
                         is_transpose=True,
                     )
+                return square
+
+            def add_feature_lanes(u, square):
                 nc.vector.tensor_reduce(
                     out=feat_sums[:, FAMILIES * u : FAMILIES * (u + 1)],
                     in_=square[:].rearrange("r (h i) -> r h i", i=LANES),
@@ -272,62 +287,95 @@ def tile_prototypelearnerv4_pa_t_kernel(
                     op=ADD,
                 )
 
-            def small_tables():
+            def permute_weight():
+                nc.vector.tensor_copy(
+                    out=u2_words[:].rearrange("k (t q b) -> k q t b", t=PACK, b=2),
+                    in_=words[:, W_U2, :].rearrange("k (q t b) -> k q t b", t=PACK, b=2),
+                )
+                nc.vector.tensor_copy(
+                    out=u2_planes[:].rearrange("k (t q) -> k q t", t=PACK),
+                    in_=planes[:, W_U2, :].rearrange("k (q t) -> k q t", t=PACK),
+                )
+
+            def bias_table():
                 bias_t = flips.tile([P, P], BF16, tag="flip")
                 nc.tensor.transpose(bias_t[:], bias_rows[:].rearrange("c h i -> c (h i)"), ident_bf[:])
                 nc.vector.tensor_copy(out=bias_cols[:], in_=bias_t[:, 0 : 2 * CHUNKS])
-                for first in range(0, CHUNKS, BANK_SQUARES):
-                    proto_wide = work.tile([P, 2, BANK_SQUARES, FAMILIES, LANES], BF16, tag="proto_wide")
-                    some = proto_rows[:, :, LANES * first : LANES * (first + BANK_SQUARES)]
-                    for h in range(FAMILIES):
-                        nc.vector.tensor_copy(out=proto_wide[:, :, :, h, :], in_=some.rearrange("p s (c i) -> p s c i", i=LANES))
-                    chunk_t = flips.tile([P, BANK_SQUARES, 2 * P], BF16, tag="flip")
-                    for n in range(BANK_SQUARES):
-                        for half in range(2):
-                            nc.tensor.transpose(
-                                chunk_t[:, n, P * half : P * (half + 1)],
-                                proto_wide[:, half, n, :, :].rearrange("p h i -> p (h i)"),
-                                ident_bf[:],
-                            )
-                    nc.vector.tensor_copy(out=proto_signed[:, first : first + BANK_SQUARES, :], in_=chunk_t[:, :, 0:PROTOS])
-                mine = proto_signed[:, 0:SCALARS, :]
-                nc.vector.tensor_scalar(out=mine, in0=mine, scalar1=-1.0, scalar2=None, op0=MULT)
+
+            def prototype_tables():
+                flipped = flips.tile([P, D // P, 2 * P], BF16, tag="flip")
+                for s in range(D // P):
+                    for half in range(2):
+                        nc.tensor.transpose(
+                            flipped[:, s, P * half : P * (half + 1)], proto_rows[:, half, P * s : P * (s + 1)], ident_bf[:]
+                        )
+                nc.vector.tensor_copy(out=proto_t[:], in_=flipped[:])
+                for first in range(0, CHUNKS, 2):
+                    selected = flips.tile([P, 2, 2 * P], F32, tag="flip")
+                    for n in range(2):
+                        c = first + n
+                        nc.tensor.matmul(
+                            out=selected[:, n, 0:PROTOS],
+                            lhsT=select[:, c % FAMILIES, :, :].rearrange("k h i -> k (h i)"),
+                            rhs=proto_t[:, c // FAMILIES, 0:PROTOS],
+                            start=True,
+                            stop=True,
+                        )
+                    mine = proto_signed[:, first : first + 2, :]
+                    if first < SCALARS:
+                        nc.scalar.mul(out=mine, in_=selected[:, :, 0:PROTOS], mul=-1.0)
+                    else:
+                        nc.vector.tensor_copy(out=mine, in_=selected[:, :, 0:PROTOS])
                 nc.vector.tensor_copy(out=proto_first[:], in_=proto_signed[:, SCALARS, :])
                 bracket_ps = flips.tile([P, PROTOS], F32, tag="flip")
-                for c in range(CHUNKS):
+                for s in range(D // P):
                     nc.tensor.matmul(
                         out=bracket_ps[:],
-                        lhsT=ones[:],
-                        rhs=proto_signed[:, c, :],
-                        start=(c == 0),
-                        stop=(c == CHUNKS - 1),
+                        lhsT=signs[:, s, :],
+                        rhs=proto_t[:, s, 0:PROTOS],
+                        start=(s == 0),
+                        stop=(s == D // P - 1),
                     )
                 nc.vector.tensor_scalar(
-                    out=bracket[:], in0=bracket_ps[:], scalar1=-1.0 / (2 * LANES * FAMILIES), scalar2=None, op0=MULT
+                    out=bracket[:], in0=bracket_ps[:], scalar1=-1.0 / (2 * LANES), scalar2=None, op0=MULT
                 )
 
+            front.enter_context(tc.manual_schedule())
+            z = {0: add_up(0)}
+            permute_weight()
             quantised = {}
             second = {}
             streams = {}
-            for step in range(GROUPS + 3):
+            for step in range(GROUPS + 4):
                 if step + 1 < GROUPS:
                     fetched[step + 1] = fetch(step + 1)
-                if step >= 3 and (step - 3) % HALVES == HALVES - 1:
-                    u = (step - 3) // HALVES
-                    make_features(u, streams[u])
-                    add_features(u)
+                if 0 <= step - 1 < GROUPS:
+                    u2_grouped = make_u2(quantised[step - 1][0])
+                if step < GROUPS:
+                    z_grouped, x_grouped = flip(step, z[step])
+                if step + 1 < GROUPS:
+                    z[step + 1] = add_up(step + 1)
+                if 0 <= step - 1 < GROUPS:
+                    second[step - 1] = quantise(u2_grouped, "u2")
+                if step == 0:
+                    bias_table()
+                square = None
+                if step >= 4:
+                    u, half = divmod(step - 4, 2)
+                    make_features(u, half, streams[u])
+                    if half == 1:
+                        square = add_features(u)
+                if step < GROUPS:
+                    quantised[step] = (quantise(z_grouped, "z"), quantise(x_grouped, "x"))
+                if step == 2:
+                    prototype_tables()
                 if 0 <= step - 2 < GROUPS:
                     g = step - 2
-                    u = g // HALVES
                     if g % HALVES == 0:
-                        streams[u] = stream_tiles()
-                    make_streams(g, second[g], quantised[g][1], streams[u])
-                if 0 <= step - 1 < GROUPS:
-                    second[step - 1] = make_u2(quantised[step - 1][0])
-                if step < GROUPS:
-                    quantised[step] = sum_and_flip(step)
-                if step == 0:
-                    small_tables()
+                        streams[g // HALVES] = stream_tiles()
+                    make_streams(g, second[g], quantised[g][1], streams[g // HALVES])
+                if square is not None:
+                    add_feature_lanes(u, square)
 
         with ExitStack() as distances:
             scalar_pieces = distances.enter_context(tc.tile_pool(name="scalar_pieces", bufs=20))
@@ -421,7 +469,7 @@ def tile_prototypelearnerv4_pa_t_kernel(
             def store(first_p, end_p):
                 nc.sync.dma_start(out=out_rows[:, :, first_p:end_p], in_=sums[:, :, first_p:end_p])
 
-            EARLY = 104
+            PARTS = (0, 104, 176, PROTOS)
             SLICE = 4
             WARM_EVERY = 2
             WARM_FIRST = 6
@@ -440,14 +488,15 @@ def tile_prototypelearnerv4_pa_t_kernel(
                 if full is not None:
                     add_lanes(full[0], full[1], slot)
                 transpose_pieces(pieces, lanes, slot)
-                late = p - EARLY - SET
-                if 0 <= late < TILES // SLICE:
-                    finish(0, EARLY, SLICE * late, SLICE * (late + 1))
-                if late == TILES // SLICE:
-                    store(0, EARLY)
+                for first_p, end_p in zip(PARTS, PARTS[1:-1]):
+                    late = p - end_p - SET
+                    if 0 <= late < TILES // SLICE:
+                        finish(first_p, end_p, SLICE * late, SLICE * (late + 1))
+                    if late == TILES // SLICE:
+                        store(first_p, end_p)
                 if slot == SET - 1:
                     full = (p - slot, lanes)
             for u in range(UNITS):
                 add_lanes(full[0], full[1], u)
-            finish(EARLY, PROTOS, 0, TILES)
-            store(EARLY, PROTOS)
+            finish(PARTS[-2], PROTOS, 0, TILES)
+            store(PARTS[-2], PROTOS)

@@ -12,6 +12,7 @@ FP8X4 = mybir.dt.float8_e4m3fn_x4
 FP4X4 = mybir.dt.float4_e2m1fn_x4
 ADD = mybir.AluOpType.add
 MAX = mybir.AluOpType.max
+MIN = mybir.AluOpType.min
 MULT = mybir.AluOpType.mult
 RELU = mybir.ActivationFunctionType.Relu
 
@@ -29,6 +30,7 @@ COLS = UNITS * P
 GROUP = 4
 GROUP_COLS = GROUP * P
 GROUPS = TILES // GROUP
+FLOAT32_MAX = 3.4028234663852886e38
 SET = 4
 HALVES = FAMILIES // GROUP
 BANK_SQUARES = 4
@@ -37,9 +39,14 @@ A_W, W_U2, W_U3 = 0, 1, 2
 QUADRANT = 32
 QUADRANT_SCALES = 4
 
-SCALARS = 14
-BEGUN = 11
-ADDED = CHUNKS - SCALARS - BEGUN
+SCALARS = (14, 13)
+FIRST = max(SCALARS)
+ADDED = 4
+GUESTS = 2
+RESIDENTS = 2
+RESIDENT_CHUNK = CHUNKS - RESIDENTS
+GUEST_CHUNK = RESIDENT_CHUNK - GUESTS
+GUEST_SECOND = GUEST_CHUNK - GUESTS
 
 FLOPS = 3 * 2 * BATCH * D * D + 3 * BATCH * PROTOS * D
 
@@ -79,7 +86,7 @@ def tile_prototypelearnerv4_pa_t_kernel(
             u2_words = once.tile([P, 2 * D], U8, align_bytes=64)
             u2_planes = once.tile([P, D], U8, align_bytes=64)
             ident_bf = once.tile([P, P], BF16)
-            signs = once.tile([P, D // P, P], BF16)
+            signs = once.tile([P, len(SCALARS), D // P, P], BF16)
             select = once.tile([P, FAMILIES, FAMILIES, LANES], BF16)
             proto_t = once.tile([P, D // P, 2 * P], BF16)
             bu2_cols = once.tile([P, PACK], BF16)
@@ -104,12 +111,13 @@ def tile_prototypelearnerv4_pa_t_kernel(
             nc.gpsimd.memset(proto_rows[:], 0.0)
             make_identity(nc, ident_bf[:])
             make_identity(nc, ident_f[:])
-            for s in range(D // P):
-                negative = min(max(SCALARS * LANES - P * s, 0), P)
-                if negative < P:
-                    nc.gpsimd.memset(signs[:, s, :], 1.0)
-                if negative > 0:
-                    nc.gpsimd.memset(signs[0:negative, s, :], -1.0)
+            for parity, scalars in enumerate(SCALARS):
+                for s in range(D // P):
+                    negative = min(max(scalars * LANES - P * s, 0), P)
+                    if negative < P:
+                        nc.gpsimd.memset(signs[:, parity, s, :], 1.0)
+                    if negative > 0:
+                        nc.gpsimd.memset(signs[0:negative, parity, s, :], -1.0)
             for h in range(FAMILIES):
                 nc.gpsimd.tensor_copy(out=select[:, :, h, :], in_=ident_bf[:].rearrange("k (v i) -> k v i", i=LANES))
 
@@ -322,23 +330,33 @@ def tile_prototypelearnerv4_pa_t_kernel(
                             stop=True,
                         )
                     mine = proto_signed[:, first : first + 2, :]
-                    if first < SCALARS:
+                    if first < FIRST:
                         nc.scalar.mul(out=mine, in_=selected[:, :, 0:PROTOS], mul=-1.0)
                     else:
                         nc.vector.tensor_copy(out=mine, in_=selected[:, :, 0:PROTOS])
-                nc.vector.tensor_copy(out=proto_first[:], in_=proto_signed[:, SCALARS, :])
-                bracket_ps = flips.tile([P, PROTOS], F32, tag="flip")
-                for s in range(D // P):
-                    nc.tensor.matmul(
-                        out=bracket_ps[:],
-                        lhsT=signs[:, s, :],
-                        rhs=proto_t[:, s, 0:PROTOS],
-                        start=(s == 0),
-                        stop=(s == D // P - 1),
+                for parity, scalars in enumerate(SCALARS):
+                    if scalars < FIRST:
+                        mine = proto_signed[:, scalars:FIRST, parity : PROTOS : len(SCALARS)]
+                        nc.vector.tensor_scalar(out=mine, in0=mine, scalar1=-1.0, scalar2=None, op0=MULT)
+                nc.vector.tensor_copy(out=proto_first[:], in_=proto_signed[:, FIRST, :])
+                for parity in range(len(SCALARS)):
+                    bracket_ps = flips.tile([P, PROTOS], F32, tag="flip")
+                    for s in range(D // P):
+                        nc.tensor.matmul(
+                            out=bracket_ps[:],
+                            lhsT=signs[:, parity, s, :],
+                            rhs=proto_t[:, s, 0:PROTOS],
+                            start=(s == 0),
+                            stop=(s == D // P - 1),
+                        )
+                    columns = slice(parity, PROTOS, len(SCALARS))
+                    nc.vector.tensor_scalar(
+                        out=bracket[:, columns],
+                        in0=bracket_ps[:, columns],
+                        scalar1=-1.0 / (2 * LANES),
+                        scalar2=None,
+                        op0=MULT,
                     )
-                nc.vector.tensor_scalar(
-                    out=bracket[:], in0=bracket_ps[:], scalar1=-1.0 / (2 * LANES), scalar2=None, op0=MULT
-                )
 
             front.enter_context(tc.manual_schedule())
             z = {0: add_up(0)}
@@ -381,14 +399,39 @@ def tile_prototypelearnerv4_pa_t_kernel(
             scalar_pieces = distances.enter_context(tc.tile_pool(name="scalar_pieces", bufs=20))
             vector_pieces = distances.enter_context(tc.tile_pool(name="vector_pieces", bufs=20))
             results = distances.enter_context(tc.tile_pool(name="results", bufs=1))
-            banks = distances.enter_context(tc.psum_pool(name="banks", bufs=2))
+            banks = distances.enter_context(tc.psum_pool(name="banks", bufs=6))
+            residents = distances.enter_context(tc.psum_pool(name="residents", bufs=1))
             sums = results.tile([P, TILES, PROTOS], F32)
             distances.enter_context(tc.manual_schedule())
 
-            def begin(p, n):
-                c = SCALARS + n
+            def make_resident(k):
+                bank = residents.tile([P, COLS], F32, tag="resident_%d" % k)
+                turned = results.tile([P, COLS], F32, tag="turned_%d" % k)
+                for u in range(UNITS):
+                    cols = slice(P * u, P * (u + 1))
+                    nc.tensor.transpose(bank[:, cols], feat[:, RESIDENT_CHUNK + k, cols], ident_f[:])
+                nc.scalar.copy(out=turned[:], in_=bank[:])
+                for u in range(UNITS):
+                    cols = slice(P * u, P * (u + 1))
+                    nc.tensor.transpose(bank[:, cols], turned[:, cols], ident_f[:])
+                return bank
+
+            def invite(p, k):
+                c = GUEST_CHUNK + k
+                guest = results.tile([P, COLS], F32, tag="guest_%d" % k)
+                nc.gpsimd.tensor_scalar(
+                    out=guest[:],
+                    in0=feat[:, c, :],
+                    scalar1=FLOAT32_MAX,
+                    scalar2=proto_signed[:, c, p : p + 1],
+                    op0=MIN,
+                    op1=MAX,
+                )
+                return guest
+
+            def begin(p, c):
                 piece = vector_pieces.tile([P, COLS], F32, tag="vector_piece")
-                if n == 0:
+                if c == FIRST:
                     nc.vector.tensor_scalar(
                         out=piece[:],
                         in0=feat[:, c, :],
@@ -403,38 +446,61 @@ def tile_prototypelearnerv4_pa_t_kernel(
                     )
                 return piece
 
-            def add_chunk(p, piece, c):
+            def add_chunk(p, c, features, piece, longer):
                 nc.vector.scalar_tensor_tensor(
-                    out=piece[:],
-                    in0=feat[:, c, :],
+                    out=longer[:],
+                    in0=features,
                     scalar=proto_signed[:, c, p : p + 1],
                     in1=piece[:],
                     op0=MAX,
                     op1=ADD,
                 )
 
-            def prepare(p):
-                scalar_made = []
-                for c in range(SCALARS):
+            def prepare(p, guests, to_reduce):
+                scalars = SCALARS[p % len(SCALARS)]
+                made = []
+                for c in range(scalars):
                     piece = scalar_pieces.tile([P, COLS], F32, tag="scalar_piece")
                     nc.scalar.activation(out=piece[:], in_=feat[:, c, :], func=RELU, bias=proto_signed[:, c, p : p + 1])
-                    scalar_made.append(((2 * c + 1) / SCALARS, piece))
-                vector_made = []
-                added = 0
-                for n in range(BEGUN + 1):
-                    if n < BEGUN:
-                        piece = begin(p, n)
-                        vector_made.append(((2 * n + 1) / BEGUN, piece))
-                    if n > 0 and n * ADDED // BEGUN > added:
-                        add_chunk(p, vector_made[n - 1][1], SCALARS + BEGUN + added)
-                        added += 1
-                return [piece for place, piece in sorted(scalar_made + vector_made, key=lambda made: made[0])]
+                    made.append(((c + 1) / scalars, piece))
+                own = [FIRST] + [c for c in range(scalars, GUEST_SECOND) if c != FIRST]
+                begun, added = own[:-ADDED], own[-ADDED:]
+                whole_work = len(begun) + 2 * (ADDED + GUESTS + RESIDENTS + 1)
+                work = 0
+                mine = []
+                for n, c in enumerate(begun):
+                    mine.append(begin(p, c))
+                    work += 1
+                    if 0 < n <= ADDED:
+                        add_chunk(p, added[n - 1], feat[:, added[n - 1], :], mine[n - 1], mine[n - 1])
+                        work += 2
+                        made.append((work / whole_work, mine[n - 1]))
+                    if ADDED <= n < len(begun) - RESIDENTS:
+                        made.append((work / whole_work, mine[n]))
+                for k in range(GUESTS):
+                    c = GUEST_SECOND + k
+                    longer = vector_pieces.tile([P, COLS], F32, tag="vector_piece")
+                    add_chunk(p, c, feat[:, c, :], guests[k], longer)
+                    work += 2
+                    made.append((work / whole_work, longer))
+                following = {}
+                if p + 1 < PROTOS:
+                    for k in reversed(range(GUESTS)):
+                        following[k] = invite(p + 1, k)
+                for k in range(RESIDENTS):
+                    piece = mine[len(begun) - RESIDENTS + k]
+                    add_chunk(p, RESIDENT_CHUNK + k, resident[k][:], piece, piece)
+                    work += 2
+                    made.append((work / whole_work, piece))
+                if to_reduce is not None:
+                    add_lanes(*to_reduce)
+                return [piece for place, piece in sorted(made, key=lambda entry: entry[0])], following
 
-            def transpose_pieces(pieces, lanes, slot):
+            def transpose_pieces(p, pieces, lanes):
                 for k, piece in enumerate(pieces):
                     for u in range(UNITS):
                         nc.tensor.matmul(
-                            out=lanes[u][:, slot, :],
+                            out=lanes[u][:, (p - u) % SET, :],
                             lhsT=piece[:, P * u : P * (u + 1)],
                             rhs=ident_f[:],
                             start=(k == 0),
@@ -442,14 +508,15 @@ def tile_prototypelearnerv4_pa_t_kernel(
                             is_transpose=True,
                         )
 
-            def keep_warm(lanes, count):
+            def keep_warm(bank, count):
                 for n in range(count):
-                    nc.tensor.matmul(out=lanes[0][:, SET - 1, :], lhsT=ident_f[:], rhs=ident_f[:], start=True, stop=True)
+                    nc.tensor.matmul(out=bank[:, SET - 1, :], lhsT=ident_f[:], rhs=ident_f[:], start=True, stop=True)
 
-            def add_lanes(first_p, lanes, u):
+            def add_lanes(u, bank, first_p, end_p):
+                slot = (first_p - u) % SET
                 nc.vector.tensor_reduce(
-                    out=sums[:, FAMILIES * u : FAMILIES * (u + 1), first_p : first_p + SET].rearrange("r h s -> r s h"),
-                    in_=lanes[u][:].rearrange("r s (h i) -> r s h i", i=LANES),
+                    out=sums[:, FAMILIES * u : FAMILIES * (u + 1), first_p:end_p].rearrange("r h s -> r s h"),
+                    in_=bank[:, slot : slot + end_p - first_p, :].rearrange("r s (h i) -> r s h i", i=LANES),
                     axis=mybir.AxisListType.X,
                     op=ADD,
                 )
@@ -471,32 +538,37 @@ def tile_prototypelearnerv4_pa_t_kernel(
 
             PARTS = (0, 104, 176, PROTOS)
             SLICE = 4
-            WARM_EVERY = 2
+            WARM_EVERY = 20
             WARM_FIRST = 6
             WARM_LATER = 3
+            guests = {}
+            for k in range(GUESTS):
+                guests[k] = invite(0, k)
+            resident = []
+            for k in range(RESIDENTS):
+                resident.append(make_resident(k))
+            lanes = {}
+            begins = {}
             full = None
             for p in range(PROTOS):
-                slot = p % SET
-                if slot == 0:
-                    lanes = []
-                    for u in range(UNITS):
-                        bank = banks.tile([P, SET, P], F32, tag="lanes_%d" % u)
-                        lanes.append(bank)
-                    if p // SET % WARM_EVERY == 0:
-                        keep_warm(lanes, WARM_FIRST if p == 0 else WARM_LATER)
-                pieces = prepare(p)
-                if full is not None:
-                    add_lanes(full[0], full[1], slot)
-                transpose_pieces(pieces, lanes, slot)
+                for u in range(UNITS):
+                    if p == 0 or (p - u) % SET == 0:
+                        bank = banks.tile([P, SET, P], F32, tag="lanes")
+                        lanes[u] = bank
+                        begins[u] = p
+                if p % WARM_EVERY == 0:
+                    keep_warm(lanes[0], WARM_FIRST if p == 0 else WARM_LATER)
+                pieces, guests = prepare(p, guests, full)
+                transpose_pieces(p, pieces, lanes)
                 for first_p, end_p in zip(PARTS, PARTS[1:-1]):
-                    late = p - end_p - SET
+                    late = p - end_p - SET - 1
                     if 0 <= late < TILES // SLICE:
                         finish(first_p, end_p, SLICE * late, SLICE * (late + 1))
                     if late == TILES // SLICE:
                         store(first_p, end_p)
-                if slot == SET - 1:
-                    full = (p - slot, lanes)
+                u = (p + 1) % SET
+                full = (u, lanes[u], begins[u], p + 1)
             for u in range(UNITS):
-                add_lanes(full[0], full[1], u)
+                add_lanes(u, lanes[u], begins[u], PROTOS)
             finish(PARTS[-2], PROTOS, 0, TILES)
             store(PARTS[-2], PROTOS)

@@ -41,9 +41,9 @@ QUADRANT_SCALES = 4
 
 SCALARS = (14, 13)
 FIRST = max(SCALARS)
-ADDED = 4
+ADDED = 3
 GUESTS = 2
-RESIDENTS = 2
+RESIDENTS = 3
 RESIDENT_CHUNK = CHUNKS - RESIDENTS
 GUEST_CHUNK = RESIDENT_CHUNK - GUESTS
 GUEST_SECOND = GUEST_CHUNK - GUESTS
@@ -399,7 +399,7 @@ def tile_prototypelearnerv4_pa_t_kernel(
             scalar_pieces = distances.enter_context(tc.tile_pool(name="scalar_pieces", bufs=20))
             vector_pieces = distances.enter_context(tc.tile_pool(name="vector_pieces", bufs=20))
             results = distances.enter_context(tc.tile_pool(name="results", bufs=1))
-            banks = distances.enter_context(tc.psum_pool(name="banks", bufs=6))
+            banks = distances.enter_context(tc.psum_pool(name="banks", bufs=5))
             residents = distances.enter_context(tc.psum_pool(name="residents", bufs=1))
             sums = results.tile([P, TILES, PROTOS], F32)
             distances.enter_context(tc.manual_schedule())

from contextlib import ExitStack

import concourse.mybir as mybir
from concourse.masks import make_identity

F32 = mybir.dt.float32
BF16 = mybir.dt.bfloat16
I32 = mybir.dt.int32
U32 = mybir.dt.uint32
U8 = mybir.dt.uint8
FP8X4 = mybir.dt.float8_e4m3fn_x4
FP4X4 = mybir.dt.float4_e2m1fn_x4
ADD = mybir.AluOpType.add
MAX = mybir.AluOpType.max
MIN = mybir.AluOpType.min
MULT = mybir.AluOpType.mult
RELU = mybir.ActivationFunctionType.Relu

P = 128
PACK = 4
BATCH = 4096
D = 512
PROTOS = 200
TILES = BATCH // P
FAMILIES = 8
LANES = P // FAMILIES
CHUNKS = D // LANES
UNITS = TILES // FAMILIES
COLS = UNITS * P
GROUP = 4
GROUP_COLS = GROUP * P
GROUPS = TILES // GROUP
FLOAT32_MAX = 3.4028234663852886e38
SET = 4
HALVES = FAMILIES // GROUP
BANK_SQUARES = 4
WEIGHTS = 3
A_W, W_U2, W_U3 = 0, 1, 2
QUADRANT = 32
QUADRANT_SCALES = 4

SCALARS = (14, 13)
FIRST = max(SCALARS)
ADDED = 3
GUESTS = 2
RESIDENTS = 3
RESIDENT_CHUNK = CHUNKS - RESIDENTS
GUEST_CHUNK = RESIDENT_CHUNK - GUESTS
GUEST_SECOND = GUEST_CHUNK - GUESTS

FLOPS = 3 * 2 * BATCH * D * D + 3 * BATCH * PROTOS * D


def tile_prototypelearnerv4_pa_t_kernel(
    tc, x, aW_words, aW_scales, ab, h_up, h_skip, Wu2_words, Wu2_scales, bu2, Wu3_words, Wu3_scales, bu3, protos, out
):
    nc = tc.nc
    by_tile = "(r i) d -> r i d"
    x_rows = x.rearrange(by_tile, i=TILES)
    h_up_rows = h_up.rearrange(by_tile, i=TILES)
    h_skip_rows = h_skip.rearrange(by_tile, i=TILES)
    out_rows = out.rearrange(by_tile, i=TILES)

    with ExitStack() as whole:
        keep = whole.enter_context(tc.tile_pool(name="keep", bufs=1))
        feat = keep.tile([P, CHUNKS, COLS], F32)
        ident_f = keep.tile([P, P], F32)
        proto_signed = keep.tile([P, CHUNKS, PROTOS], BF16)
        proto_first = keep.tile([P, PROTOS], F32)
        bracket = keep.tile([P, PROTOS], F32)
        feat_sums = keep.tile([P, TILES], F32)

        with ExitStack() as front:
            once = front.enter_context(tc.tile_pool(name="once", bufs=1))
            loads = front.enter_context(tc.tile_pool(name="loads", bufs=2))
            x_loads = front.enter_context(tc.tile_pool(name="x_loads", bufs=4))
            work = front.enter_context(tc.tile_pool(name="work", bufs=2))
            stream_pool = front.enter_context(tc.tile_pool(name="streams", bufs=3))
            grouped_tiles = front.enter_context(tc.tile_pool(name="grouped_tiles", bufs=2))
            operands = front.enter_context(tc.tile_pool(name="operands", bufs=3))
            flips = front.enter_context(tc.psum_pool(name="flips", bufs=4))
            products = front.enter_context(tc.psum_pool(name="products", bufs=4))

            words = once.tile([P, WEIGHTS, 2 * D], U8, align_bytes=64)
            planes = once.tile([P, WEIGHTS, D], U8, align_bytes=64)
            u2_words = once.tile([P, 2 * D], U8, align_bytes=64)
            u2_planes = once.tile([P, D], U8, align_bytes=64)
            ident_bf = once.tile([P, P], BF16)
            signs = once.tile([P, len(SCALARS), D // P, P], BF16)
            select = once.tile([P, FAMILIES, FAMILIES, LANES], BF16)
            proto_t = once.tile([P, D // P, 2 * P], BF16)
            bu2_cols = once.tile([P, PACK], BF16)
            bias_rows = once.tile([P, FAMILIES, LANES], BF16)
            bias_cols = once.tile([P, 2 * CHUNKS], F32)
            proto_rows = once.tile([P, 2, D], BF16)

            def fetch(g):
                rows = slice(GROUP * g, GROUP * (g + 1))
                hu = loads.tile([P, GROUP, D], BF16, tag="hu")
                hs = loads.tile([P, GROUP, D], BF16, tag="hs")
                xs = x_loads.tile([P, GROUP, D], BF16, tag="xs")
                nc.sync.dma_start(out=hu[:], in_=h_up_rows[:, rows, :])
                nc.sync.dma_start(out=hs[:], in_=h_skip_rows[:, rows, :])
                nc.sync.dma_start(out=xs[:], in_=x_rows[:, rows, :])
                return hu, hs, xs

            fetched = {0: fetch(0)}

            nc.vector.memset(planes[:].rearrange("q w n -> q (w n)").bitcast(I32), 0)
            nc.gpsimd.memset(bias_rows[:], 0.0)
            nc.gpsimd.memset(proto_rows[:], 0.0)
            make_identity(nc, ident_bf[:])
            make_identity(nc, ident_f[:])
            for parity, scalars in enumerate(SCALARS):
                for s in range(D // P):
                    negative = min(max(scalars * LANES - P * s, 0), P)
                    if negative < P:
                        nc.gpsimd.memset(signs[:, parity, s, :], 1.0)
                    if negative > 0:
                        nc.gpsimd.memset(signs[0:negative, parity, s, :], -1.0)
            for h in range(FAMILIES):
                nc.gpsimd.tensor_copy(out=select[:, :, h, :], in_=ident_bf[:].rearrange("k (v i) -> k v i", i=LANES))

            given = ((W_U2, Wu2_words, Wu2_scales), (W_U3, Wu3_words, Wu3_scales), (A_W, aW_words, aW_scales))
            for w, w_words, w_scales in given:
                nc.sync.dma_start(out=words[:, w, :].bitcast(I32), in_=w_words[0].bitcast(I32))
            for w, w_words, w_scales in given:
                for quad in range(P // QUADRANT):
                    nc.sync.dma_start(
                        out=planes[QUADRANT * quad : QUADRANT * quad + QUADRANT_SCALES, w, :].bitcast(I32),
                        in_=w_scales[0, QUADRANT_SCALES * quad : QUADRANT_SCALES * (quad + 1), :].bitcast(I32),
                    )
            nc.scalar.dma_start(out=bu2_cols[:], in_=bu2.rearrange("(q t) -> q t", t=PACK))
            for h in range(FAMILIES):
                nc.scalar.dma_start(out=bias_rows[0:CHUNKS, h, :], in_=bu3.rearrange("(c i) -> c i", i=LANES))
                nc.scalar.dma_start(out=bias_rows[CHUNKS : 2 * CHUNKS, h, :], in_=ab.rearrange("(c i) -> c i", i=LANES))
            nc.scalar.dma_start(out=proto_rows[:, 0, :], in_=protos[0:P, :])
            nc.scalar.dma_start(out=proto_rows[0 : PROTOS - P, 1, :], in_=protos[P:PROTOS, :])

            def add_up(g):
                hu, hs, xs = fetched[g]
                z = work.tile([P, GROUP, D], BF16, tag="z")
                nc.vector.tensor_tensor(out=z[:], in0=hu[:], in1=hs[:], op=ADD)
                return z

            def flip(g, z):
                z_grouped = grouped_tiles.tile([P, GROUP_COLS, PACK], BF16, tag="z_grouped", align_bytes=64)
                for pair in range(GROUP // 2):
                    flipped = flips.tile([P, PACK, 2 * P], BF16, tag="flip")
                    for j in range(2):
                        for t in range(PACK):
                            nc.tensor.transpose(
                                flipped[:, t, P * j : P * (j + 1)], z[:, 2 * pair + j, t:D:PACK], ident_bf[:]
                            )
                    nc.scalar.copy(
                        out=z_grouped[:, 2 * P * pair : 2 * P * (pair + 1), :], in_=flipped[:].rearrange("q t b -> q b t")
                    )
                xs = fetched[g][2]
                x_grouped = grouped_tiles.tile([P, GROUP_COLS, PACK], BF16, tag="x_grouped", align_bytes=64)
                x_pairs = x_grouped[:].rearrange("q b t -> q (b t)").bitcast(F32).rearrange("q (b v) -> q b v", v=2)
                for pair in range(GROUP // 2):
                    flipped = flips.tile([P, 2, 2 * P], F32, tag="flip")
                    for j in range(2):
                        x_words = xs[:, 2 * pair + j, :].bitcast(F32)
                        for v in range(2):
                            nc.tensor.transpose(flipped[:, v, P * j : P * (j + 1)], x_words[:, v : D // 2 : 2], ident_f[:])
                    nc.scalar.copy(
                        out=x_pairs[:, 2 * P * pair : 2 * P * (pair + 1), :], in_=flipped[:].rearrange("q v b -> q b v")
                    )
                return z_grouped, x_grouped

            def quantise(grouped, name):
                codes = operands.tile([P, GROUP_COLS], U32, tag="codes_" + name, align_bytes=64)
                scales = operands.tile([P, GROUP_COLS], U8, tag="scales_" + name, align_bytes=64)
                nc.vector.quantize_mx(
                    out=codes[:].bitcast(FP8X4), scales=scales[:], in_=grouped[:].rearrange("q b t -> q (b t)")
                )
                return codes, scales

            def make_u2(z_quantised):
                z_codes, z_scales = z_quantised
                u2_grouped = grouped_tiles.tile([P, GROUP_COLS, PACK], BF16, tag="u2_grouped", align_bytes=64)
                for j in range(GROUP):
                    rows = slice(P * j, P * (j + 1))
                    product = products.tile([P, PACK, P], F32, tag="product")
                    for t in range(PACK):
                        nc.tensor.matmul_mx(
                            out=product[:, t, :],
                            lhsT=u2_words[:, 2 * P * t : 2 * P * (t + 1)].bitcast(FP4X4),
                            lhsT_scale=u2_planes[:, P * t : P * (t + 1)],
                            rhs=z_codes[:, rows].bitcast(FP8X4),
                            rhs_scale=z_scales[:, rows],
                            start=True,
                            stop=True,
                        )
                    nc.vector.tensor_tensor(
                        out=u2_grouped[:, rows, :],
                        in0=product[:].rearrange("q t b -> q b t"),
                        in1=bu2_cols[:].unsqueeze(1).to_broadcast([P, P, PACK]),
                        op=ADD,
                    )
                flat = u2_grouped[:].rearrange("q b t -> q (b t)")
                nc.vector.tensor_scalar(out=flat, in0=flat, scalar1=0.0, scalar2=None, op0=MAX)
                return u2_grouped

            def stream_tiles():
                tiles = []
                for half in range(2):
                    up_rows = stream_pool.tile([P, CHUNKS // 2, FAMILIES, LANES], F32, tag="up_rows")
                    adapted = stream_pool.tile([P, CHUNKS // 2, FAMILIES, LANES], F32, tag="adapted")
                    tiles.append((up_rows, adapted))
                return tiles

            def make_streams(g, u2_quantised, x_quantised, tiles):
                u2_codes, u2_scales = u2_quantised
                x_codes, x_scales = x_quantised
                xs = fetched[g][2]
                for j in range(GROUP):
                    h = GROUP * (g % HALVES) + j
                    rows = slice(P * j, P * (j + 1))
                    up = products.tile([P, D], F32, tag="product")
                    nc.tensor.matmul_mx(
                        out=up[:],
                        lhsT=u2_codes[:, rows].bitcast(FP8X4),
                        lhsT_scale=u2_scales[:, rows],
                        rhs=words[:, W_U3, :].bitcast(FP4X4),
                        rhs_scale=planes[:, W_U3, :],
                        start=True,
                        stop=True,
                    )
                    adapter = products.tile([P, D], F32, tag="product")
                    nc.tensor.matmul_mx(
                        out=adapter[:],
                        lhsT=x_codes[:, rows].bitcast(FP8X4),
                        lhsT_scale=x_scales[:, rows],
                        rhs=words[:, A_W, :].bitcast(FP4X4),
                        rhs_scale=planes[:, A_W, :],
                        start=True,
                        stop=True,
                    )
                    for half in range(2):
                        up_rows, adapted = tiles[half]
                        features = slice(D // 2 * half, D // 2 * (half + 1))
                        nc.scalar.copy(out=up_rows[:, :, h, :], in_=up[:, features].rearrange("r (c i) -> r c i", i=LANES))
                        nc.vector.tensor_tensor(
                            out=adapted[:, :, h, :],
                            in0=adapter[:, features].rearrange("r (c i) -> r c i", i=LANES),
                            in1=xs[:, j, features].rearrange("r (c i) -> r c i", i=LANES),
                            op=ADD,
                        )

            def make_features(u, half, tiles):
                up_rows, adapted = tiles[half]
                cols = slice(P * u, P * (u + 1))
                for first in range(0, CHUNKS // 2, BANK_SQUARES):
                    up_t = flips.tile([P, BANK_SQUARES, P], F32, tag="flip")
                    for n in range(BANK_SQUARES):
                        nc.tensor.transpose(up_t[:, n, :], up_rows[:, first + n, :, :].rearrange("r h i -> r (h i)"), ident_f[:])
                    adapted_t = flips.tile([P, BANK_SQUARES, P], F32, tag="flip")
                    for n in range(BANK_SQUARES):
                        nc.tensor.transpose(
                            adapted_t[:, n, :], adapted[:, first + n, :, :].rearrange("r h i -> r (h i)"), ident_f[:]
                        )
                    u3 = work.tile([P, BANK_SQUARES, P], F32, tag="u3")
                    for n in range(BANK_SQUARES):
                        c = CHUNKS // 2 * half + first + n
                        nc.scalar.activation(out=u3[:, n, :], in_=up_t[:, n, :], func=RELU, bias=bias_cols[:, c : c + 1])
                        nc.vector.scalar_tensor_tensor(
                            out=feat[:, c, cols],
                            in0=adapted_t[:, n, :],
                            scalar=bias_cols[:, CHUNKS + c : CHUNKS + c + 1],
                            in1=u3[:, n, :],
                            op0=ADD,
                            op1=ADD,
                        )

            def add_features(u):
                square = flips.tile([P, P], F32, tag="flip")
                for c in range(CHUNKS):
                    nc.tensor.matmul(
                        out=square[:],
                        lhsT=feat[:, c, P * u : P * (u + 1)],
                        rhs=ident_f[:],
                        start=(c == 0),
                        stop=(c == CHUNKS - 1),
                        is_transpose=True,
                    )
                return square

            def add_feature_lanes(u, square):
                nc.vector.tensor_reduce(
                    out=feat_sums[:, FAMILIES * u : FAMILIES * (u + 1)],
                    in_=square[:].rearrange("r (h i) -> r h i", i=LANES),
                    axis=mybir.AxisListType.X,
                    op=ADD,
                )

            def permute_weight():
                nc.vector.tensor_copy(
                    out=u2_words[:].rearrange("k (t q b) -> k q t b", t=PACK, b=2),
                    in_=words[:, W_U2, :].rearrange("k (q t b) -> k q t b", t=PACK, b=2),
                )
                nc.vector.tensor_copy(
                    out=u2_planes[:].rearrange("k (t q) -> k q t", t=PACK),
                    in_=planes[:, W_U2, :].rearrange("k (q t) -> k q t", t=PACK),
                )

            def bias_table():
                bias_t = flips.tile([P, P], BF16, tag="flip")
                nc.tensor.transpose(bias_t[:], bias_rows[:].rearrange("c h i -> c (h i)"), ident_bf[:])
                nc.vector.tensor_copy(out=bias_cols[:], in_=bias_t[:, 0 : 2 * CHUNKS])

            def prototype_tables():
                flipped = flips.tile([P, D // P, 2 * P], BF16, tag="flip")
                for s in range(D // P):
                    for half in range(2):
                        nc.tensor.transpose(
                            flipped[:, s, P * half : P * (half + 1)], proto_rows[:, half, P * s : P * (s + 1)], ident_bf[:]
                        )
                nc.vector.tensor_copy(out=proto_t[:], in_=flipped[:])
                for first in range(0, CHUNKS, 2):
                    selected = flips.tile([P, 2, 2 * P], F32, tag="flip")
                    for n in range(2):
                        c = first + n
                        nc.tensor.matmul(
                            out=selected[:, n, 0:PROTOS],
                            lhsT=select[:, c % FAMILIES, :, :].rearrange("k h i -> k (h i)"),
                            rhs=proto_t[:, c // FAMILIES, 0:PROTOS],
                            start=True,
                            stop=True,
                        )
                    mine = proto_signed[:, first : first + 2, :]
                    if first < FIRST:
                        nc.scalar.mul(out=mine, in_=selected[:, :, 0:PROTOS], mul=-1.0)
                    else:
                        nc.vector.tensor_copy(out=mine, in_=selected[:, :, 0:PROTOS])
                for parity, scalars in enumerate(SCALARS):
                    if scalars < FIRST:
                        mine = proto_signed[:, scalars:FIRST, parity : PROTOS : len(SCALARS)]
                        nc.vector.tensor_scalar(out=mine, in0=mine, scalar1=-1.0, scalar2=None, op0=MULT)
                nc.vector.tensor_copy(out=proto_first[:], in_=proto_signed[:, FIRST, :])
                for parity in range(len(SCALARS)):
                    bracket_ps = flips.tile([P, PROTOS], F32, tag="flip")
                    for s in range(D // P):
                        nc.tensor.matmul(
                            out=bracket_ps[:],
                            lhsT=signs[:, parity, s, :],
                            rhs=proto_t[:, s, 0:PROTOS],
                            start=(s == 0),
                            stop=(s == D // P - 1),
                        )
                    columns = slice(parity, PROTOS, len(SCALARS))
                    nc.vector.tensor_scalar(
                        out=bracket[:, columns],
                        in0=bracket_ps[:, columns],
                        scalar1=-1.0 / (2 * LANES),
                        scalar2=None,
                        op0=MULT,
                    )

            front.enter_context(tc.manual_schedule())
            z = {0: add_up(0)}
            permute_weight()
            quantised = {}
            second = {}
            streams = {}
            for step in range(GROUPS + 4):
                if step + 1 < GROUPS:
                    fetched[step + 1] = fetch(step + 1)
                if 0 <= step - 1 < GROUPS:
                    u2_grouped = make_u2(quantised[step - 1][0])
                if step < GROUPS:
                    z_grouped, x_grouped = flip(step, z[step])
                if step + 1 < GROUPS:
                    z[step + 1] = add_up(step + 1)
                if 0 <= step - 1 < GROUPS:
                    second[step - 1] = quantise(u2_grouped, "u2")
                if step == 0:
                    bias_table()
                square = None
                if step >= 4:
                    u, half = divmod(step - 4, 2)
                    make_features(u, half, streams[u])
                    if half == 1:
                        square = add_features(u)
                if step < GROUPS:
                    quantised[step] = (quantise(z_grouped, "z"), quantise(x_grouped, "x"))
                if step == 2:
                    prototype_tables()
                if 0 <= step - 2 < GROUPS:
                    g = step - 2
                    if g % HALVES == 0:
                        streams[g // HALVES] = stream_tiles()
                    make_streams(g, second[g], quantised[g][1], streams[g // HALVES])
                if square is not None:
                    add_feature_lanes(u, square)

        with ExitStack() as distances:
            scalar_pieces = distances.enter_context(tc.tile_pool(name="scalar_pieces", bufs=20))
            vector_pieces = distances.enter_context(tc.tile_pool(name="vector_pieces", bufs=20))
            results = distances.enter_context(tc.tile_pool(name="results", bufs=1))
            banks = distances.enter_context(tc.psum_pool(name="banks", bufs=5))
            residents = distances.enter_context(tc.psum_pool(name="residents", bufs=1))
            sums = results.tile([P, TILES, PROTOS], F32)
            distances.enter_context(tc.manual_schedule())

            def make_resident(k):
                bank = residents.tile([P, COLS], F32, tag="resident_%d" % k)
                turned = results.tile([P, COLS], F32, tag="turned_%d" % k)
                for u in range(UNITS):
                    cols = slice(P * u, P * (u + 1))
                    nc.tensor.transpose(bank[:, cols], feat[:, RESIDENT_CHUNK + k, cols], ident_f[:])
                nc.scalar.copy(out=turned[:], in_=bank[:])
                for u in range(UNITS):
                    cols = slice(P * u, P * (u + 1))
                    nc.tensor.transpose(bank[:, cols], turned[:, cols], ident_f[:])
                return bank

            def invite(p, k):
                c = GUEST_CHUNK + k
                guest = results.tile([P, COLS], F32, tag="guest_%d" % k)
                nc.gpsimd.tensor_scalar(
                    out=guest[:],
                    in0=feat[:, c, :],
                    scalar1=FLOAT32_MAX,
                    scalar2=proto_signed[:, c, p : p + 1],
                    op0=MIN,
                    op1=MAX,
                )
                return guest

            def begin(p, c):
                piece = vector_pieces.tile([P, COLS], F32, tag="vector_piece")
                if c == FIRST:
                    nc.vector.tensor_scalar(
                        out=piece[:],
                        in0=feat[:, c, :],
                        scalar1=proto_first[:, p : p + 1],
                        scalar2=bracket[:, p : p + 1],
                        op0=MAX,
                        op1=ADD,
                    )
                else:
                    nc.vector.tensor_scalar(
                        out=piece[:], in0=feat[:, c, :], scalar1=proto_signed[:, c, p : p + 1], scalar2=None, op0=MAX
                    )
                return piece

            def add_chunk(p, c, features, piece, longer):
                nc.vector.scalar_tensor_tensor(
                    out=longer[:],
                    in0=features,
                    scalar=proto_signed[:, c, p : p + 1],
                    in1=piece[:],
                    op0=MAX,
                    op1=ADD,
                )

            def prepare(p, guests, to_reduce):
                scalars = SCALARS[p % len(SCALARS)]
                made = []
                for c in range(scalars):
                    piece = scalar_pieces.tile([P, COLS], F32, tag="scalar_piece")
                    nc.scalar.activation(out=piece[:], in_=feat[:, c, :], func=RELU, bias=proto_signed[:, c, p : p + 1])
                    made.append(((c + 1) / scalars, piece))
                own = [FIRST] + [c for c in range(scalars, GUEST_SECOND) if c != FIRST]
                begun, added = own[:-ADDED], own[-ADDED:]
                whole_work = len(begun) + 2 * (ADDED + GUESTS + RESIDENTS + 1)
                work = 0
                mine = []
                for n, c in enumerate(begun):
                    mine.append(begin(p, c))
                    work += 1
                    if 0 < n <= ADDED:
                        add_chunk(p, added[n - 1], feat[:, added[n - 1], :], mine[n - 1], mine[n - 1])
                        work += 2
                        made.append((work / whole_work, mine[n - 1]))
                    if ADDED <= n < len(begun) - RESIDENTS:
                        made.append((work / whole_work, mine[n]))
                for k in range(GUESTS):
                    c = GUEST_SECOND + k
                    longer = vector_pieces.tile([P, COLS], F32, tag="vector_piece")
                    add_chunk(p, c, feat[:, c, :], guests[k], longer)
                    work += 2
                    made.append((work / whole_work, longer))
                following = {}
                if p + 1 < PROTOS:
                    for k in reversed(range(GUESTS)):
                        following[k] = invite(p + 1, k)
                for k in range(RESIDENTS):
                    piece = mine[len(begun) - RESIDENTS + k]
                    add_chunk(p, RESIDENT_CHUNK + k, resident[k][:], piece, piece)
                    work += 2
                    made.append((work / whole_work, piece))
                if to_reduce is not None:
                    add_lanes(*to_reduce)
                return [piece for place, piece in sorted(made, key=lambda entry: entry[0])], following

            def transpose_pieces(p, pieces, lanes):
                for k, piece in enumerate(pieces):
                    for u in range(UNITS):
                        nc.tensor.matmul(
                            out=lanes[u][:, (p - u) % SET, :],
                            lhsT=piece[:, P * u : P * (u + 1)],
                            rhs=ident_f[:],
                            start=(k == 0),
                            stop=(k == len(pieces) - 1),
                            is_transpose=True,
                        )

            def keep_warm(bank, count):
                for n in range(count):
                    nc.tensor.matmul(out=bank[:, SET - 1, :], lhsT=ident_f[:], rhs=ident_f[:], start=True, stop=True)

            def add_lanes(u, bank, first_p, end_p):
                slot = (first_p - u) % SET
                nc.vector.tensor_reduce(
                    out=sums[:, FAMILIES * u : FAMILIES * (u + 1), first_p:end_p].rearrange("r h s -> r s h"),
                    in_=bank[:, slot : slot + end_p - first_p, :].rearrange("r s (h i) -> r s h i", i=LANES),
                    axis=mybir.AxisListType.X,
                    op=ADD,
                )

            def finish(first_p, end_p, first_tile, end_tile):
                mine = sums[:, first_tile:end_tile, first_p:end_p]
                row_sums = feat_sums[:, first_tile:end_tile].unsqueeze(2)
                nc.vector.scalar_tensor_tensor(
                    out=mine,
                    in0=mine,
                    scalar=-2.0,
                    in1=row_sums.to_broadcast([P, end_tile - first_tile, end_p - first_p]),
                    op0=MULT,
                    op1=ADD,
                )

            def store(first_p, end_p):
                nc.sync.dma_start(out=out_rows[:, :, first_p:end_p], in_=sums[:, :, first_p:end_p])

            PARTS = (0, 104, 176, PROTOS)
            SLICE = 4
            WARM_EVERY = 20
            WARM_FIRST = 6
            WARM_LATER = 3
            guests = {}
            for k in range(GUESTS):
                guests[k] = invite(0, k)
            resident = []
            for k in range(RESIDENTS):
                resident.append(make_resident(k))
            lanes = {}
            begins = {}
            full = None
            for p in range(PROTOS):
                for u in range(UNITS):
                    if p == 0 or (p - u) % SET == 0:
                        bank = banks.tile([P, SET, P], F32, tag="lanes")
                        lanes[u] = bank
                        begins[u] = p
                if p % WARM_EVERY == 0:
                    keep_warm(lanes[0], WARM_FIRST if p == 0 else WARM_LATER)
                pieces, guests = prepare(p, guests, full)
                transpose_pieces(p, pieces, lanes)
                for first_p, end_p in zip(PARTS, PARTS[1:-1]):
                    late = p - end_p - SET - 1
                    if 0 <= late < TILES // SLICE:
                        finish(first_p, end_p, SLICE * late, SLICE * (late + 1))
                    if late == TILES // SLICE:
                        store(first_p, end_p)
                u = (p + 1) % SET
                full = (u, lanes[u], begins[u], p + 1)
            for u in range(UNITS):
                add_lanes(u, lanes[u], begins[u], PROTOS)
            finish(PARTS[-2], PROTOS, 0, TILES)
            store(PARTS[-2], PROTOS)
